import numpy as np
import ml_dtypes


def mxq(x, axis, fmt="e4m3"):
    dtype, down = {"e4m3": (ml_dtypes.float8_e4m3fn, 7), "e5m2": (ml_dtypes.float8_e5m2, 14)}[fmt]
    v = np.moveaxis(np.asarray(x, np.float32).astype(ml_dtypes.bfloat16).astype(np.float64), axis, -1)
    blocks = v.reshape(v.shape[:-1] + (-1, 32))
    amax = np.abs(blocks).max(-1, keepdims=True)
    byte = np.maximum(np.where(amax > 0, np.frexp(amax)[1] - 1 + 127, 0) - down, 1)
    scale = np.exp2(byte - 127.0)
    codes = (blocks / scale).astype(np.float32).astype(dtype).astype(np.float64)
    return np.moveaxis((codes * scale).reshape(v.shape), -1, axis)


WIDE = False


def mx_kscale(k):
    if not WIDE:
        return np.ones(k)
    levels = np.array([10, -10, 5, -5, 0])
    a = np.random.permutation(np.resize(levels, k // 512 * 4)).reshape(k // 512, 4)
    idx = np.arange(k)
    return np.exp2(a[idx // 512, idx % 128 // 32])


BF16 = ml_dtypes.bfloat16


def bf(x):
    return np.asarray(x, np.float32).astype(BF16)


def f64(x):
    return np.asarray(x).astype(np.float64)


E2M1 = np.array([0.0, 0.5, 1.0, 1.5, 2.0, 3.0, 4.0, 6.0, -0.0, -0.5, -1.0, -1.5, -2.0, -3.0, -4.0, -6.0])


def pack_weight(w, fmt):
    k, n = w.shape
    w = f64(bf(w)).reshape(k // 32, 32, n)
    amax = np.abs(w).max(1)
    if fmt == "e4m3":
        byte = np.frexp(amax)[1] - 1 + 127 - 7
    else:
        mant, ex = np.frexp(amax / 6.0)
        byte = np.where(mant > 0.5, ex, ex - 1) + 127
    byte = np.clip(np.where(amax > 0, byte, 1), 1, 254)
    scaled = (w * np.exp2(127.0 - byte)[:, None, :]).reshape(k, n).astype(np.float32)
    by_word = np.ascontiguousarray(scaled.reshape(k // 512, 128, 4, n).transpose(0, 1, 3, 2))
    if fmt == "e4m3":
        words = by_word.astype(ml_dtypes.float8_e4m3fn).view(np.uint8)
    else:
        c = by_word.astype(ml_dtypes.float4_e2m1fn).view(np.uint8) & 0xF
        words = c[..., 0::2] | (c[..., 1::2] << 4)
    return np.ascontiguousarray(words), np.ascontiguousarray(byte.astype(np.uint8).reshape(k // 512, 16, n))


def unpack_weight(words, scales, fmt):
    g, p, n, _ = words.shape
    if fmt == "e4m3":
        vals = np.ascontiguousarray(words).view(ml_dtypes.float8_e4m3fn).astype(np.float64)
    else:
        nib = np.empty((g, p, n, 4), np.uint8)
        nib[..., 0::2] = words & 0xF
        nib[..., 1::2] = words >> 4
        vals = E2M1[nib]
    vals = vals * np.repeat(np.exp2(scales.astype(np.float64) - 127.0), 8, axis=1)[..., None]
    return vals.transpose(0, 1, 3, 2).reshape(g * 512, n)


B, K, N, T = 128, 8192, 2560, 2
EPS = 1e-7
MAX_NORM = 1.0 - 1e-5


def _n(x):
    return np.maximum(np.sqrt(np.sum(x * x, axis=-1, keepdims=True)), EPS)


def _artanh(x):
    c = np.clip(x, -1.0 + 1e-5, 1.0 - 1e-5)
    return 0.5 * np.log((1.0 + c) / (1.0 - c))


def _project(x):
    n = _n(x)
    return x * np.where(n > MAX_NORM, MAX_NORM / n, 1.0)


def _mobius_add(x, y):
    x2 = np.sum(x * x, axis=-1, keepdims=True)
    y2 = np.sum(y * y, axis=-1, keepdims=True)
    xy = np.sum(x * y, axis=-1, keepdims=True)
    num = (1.0 + 2.0 * xy + y2) * x + (1.0 - x2) * y
    den = np.maximum(1.0 + 2.0 * xy + x2 * y2, EPS)
    return num / den


def setup_inputs():
    s = mx_kscale(K)
    g = np.sqrt(np.mean(s * s))
    m = np.random.standard_normal(K)
    w0 = np.random.standard_normal((N, K)) * 1.5 / np.sqrt(N)
    u = w0 @ m
    u = u / _n(u)
    v = (np.random.standard_normal((B, K)) + m) * s
    v = 0.7 * v / (1.0 + _n(v))
    z0 = np.random.standard_normal((B, N)) + np.random.standard_normal((B, 1)) * np.sqrt(N) * u
    z0 = 0.5 * z0 / (1.0 + _n(z0))
    b = 0.45 * (0.7 * u + 0.7 * np.random.standard_normal(N) / np.sqrt(N))
    step_sizes = np.log(2.0 / T) + 0.1 * np.random.standard_normal(1)
    W_words, W_scales = pack_weight((w0 * g / s).T, 'e4m3')
    return {'z_0': bf(z0), 'v_init': bf(v), 'W_words': W_words, 'W_scales': W_scales, 'b': bf(b), 'step_sizes': bf(step_sizes)}


def reference(z_0, v_init, W_words, W_scales, b, step_sizes):
    z_0, v_init, b, step_sizes = f64(z_0), f64(v_init), f64(b), f64(step_sizes)
    step = 1.0 / (1.0 + np.exp(-step_sizes))
    mv = mxq(v_init, 1, 'e4m3') @ unpack_weight(W_words, W_scales, 'e4m3')
    vn, mvn = _n(v_init), _n(mv)
    res = np.tanh(mvn / vn * _artanh(vn)) * mv / mvn
    bn = _n(b)
    b_pt = np.tanh(bn) * b / bn
    v0 = _project(_mobius_add(res, b_pt))
    ts = np.arange(1.0, T + 1.0)
    v_t = step * ts[None, :, None] * v0[:, None, :]
    x = z_0[:, None, :]
    lam = 2.0 / np.maximum(1.0 - np.sum(x * x, axis=-1, keepdims=True), EPS)
    vtn = _n(v_t)
    second = np.tanh(0.5 * lam * vtn) * v_t / vtn
    return _project(_mobius_add(x, second))

@@ -1,0 +1,397 @@
+from contextlib import ExitStack
+
+import concourse.mybir as mybir
+from concourse.masks import make_identity
+
+F32 = mybir.dt.float32
+BF16 = mybir.dt.bfloat16
+I32 = mybir.dt.int32
+U32 = mybir.dt.uint32
+U8 = mybir.dt.uint8
+FP8X4 = mybir.dt.float8_e4m3fn_x4
+ALU = mybir.AluOpType
+ACTF = mybir.ActivationFunctionType
+AX = mybir.AxisListType
+
+P = 128
+K = 8192
+N = 2560
+G = 16
+CH = 512
+NA = 2048
+NW = 12
+EPS = 1e-7
+EPS2 = 1e-14
+TINY = 1e-30
+MAXN = 1.0 - 1e-5
+
+FLOPS = 2 * P * K * N
+
+
+def tile_paralleldirectpoincaredynamics_w_kernel(tc, z_0, v_init, W_words, W_scales, b, step_sizes, out):
+    nc = tc.nc
+    V = nc.vector
+    A = nc.scalar
+    with ExitStack() as ctx:
+        ctx.enter_context(tc.manual_schedule())
+        keep = ctx.enter_context(tc.tile_pool(name="keep", bufs=1))
+        small = ctx.enter_context(tc.tile_pool(name="small", bufs=1))
+        wpool = ctx.enter_context(tc.tile_pool(name="wpool", bufs=NW))
+        tmpp = ctx.enter_context(tc.tile_pool(name="tmpp", bufs=5))
+        tpool = ctx.enter_context(tc.tile_pool(name="tpool", bufs=4))
+        opool = ctx.enter_context(tc.tile_pool(name="opool", bufs=10))
+        psum = ctx.enter_context(tc.psum_pool(name="psum", bufs=1))
+
+        def sm(name, cols=1):
+            return small.tile([P, cols], F32, name=name)
+
+        def ts(o, i, s1, s2, op0, op1=None):
+            if op1 is None:
+                V.tensor_scalar(out=o, in0=i, scalar1=s1, scalar2=None, op0=op0)
+            else:
+                V.tensor_scalar(out=o, in0=i, scalar1=s1, scalar2=s2, op0=op0, op1=op1)
+
+        def stt(o, i0, s, i1, op0, op1, acc=None):
+            V.scalar_tensor_tensor(out=o, in0=i0, scalar=s, in1=i1, op0=op0, op1=op1, accum_out=acc)
+
+        def tt(o, i0, i1, op):
+            V.tensor_tensor(out=o, in0=i0, in1=i1, op=op)
+
+        v_sb = keep.tile([P, K], BF16, name="v_sb", align_bytes=64)
+        grouped = keep.tile([P, G, P, 2], F32, name="grouped", align_bytes=64)
+        vcodes = keep.tile([P, G, P], U32, name="vcodes", align_bytes=64)
+        vscl = keep.tile([P, G, P], U8, name="vscl", align_bytes=64)
+        planes = keep.tile([P, 4, N], U8, name="planes", align_bytes=64)
+        ident = keep.tile([P, P], F32, name="ident")
+        ones = keep.tile([P, P], BF16, name="ones")
+        bz = keep.tile([P, N], BF16, name="bz")
+        bbc = keep.tile([P, N], BF16, name="bbc")
+        z0 = keep.tile([P, N], BF16, name="z0")
+        w = keep.tile([P, N], F32, name="w")
+        junk_a = keep.tile([P, N], BF16, name="junk_a")
+        junk_v = keep.tile([P, CH], F32, name="junk_v")
+        ssb = small.tile([P, 1], BF16, name="ssb")
+        mh = sm("mh", 2)
+        tiny = sm("tiny", 1)
+
+        for i in range(4):
+            nc.sync.dma_start(out=v_sb[:, 2048 * i:2048 * (i + 1)], in_=v_init[:, 2048 * i:2048 * (i + 1)])
+        V.memset(planes[:].rearrange("p j n -> p (j n)").bitcast(I32), 0)
+        V.memset(bz[:].bitcast(I32), 0)
+        V.memset(ones[:], 1.0)
+        V.memset(mh[:], -0.5)
+        V.memset(tiny[:], TINY)
+        make_identity(nc, ident[:])
+        A.dma_start(out=ssb[:], in_=step_sizes.partition_broadcast(P))
+        A.dma_start(out=bz[0:1, :], in_=b.rearrange("(o n) -> o n", o=1))
+        for jj in range(4):
+            for q in range(4):
+                nc.sync.dma_start(
+                    out=planes[32 * q:32 * q + 16, jj, :].bitcast(I32),
+                    in_=W_scales[4 * jj:4 * jj + 4, 4 * q:4 * q + 4, :].bitcast(I32),
+                )
+        nc.sync.dma_start(out=z0[:], in_=z_0)
+
+        wtiles = []
+
+        def load_w(n):
+            wt = wpool.tile([P, NA], U32, name="wt%d" % n, tag="wt", align_bytes=64)
+            wtiles.append(wt)
+            dst = wt[:].bitcast(I32)
+            if n < G:
+                src = W_words[n].rearrange("p n t -> p (n t)")[:, 0:4 * NA].bitcast(I32)
+                nc.sync.dma_start(out=dst, in_=src)
+            else:
+                g0 = 4 * (n - G)
+                cuts = [(0, 4)] if n < G + 3 else [(0, 2), (2, 3), (3, 4)]
+                dst3 = dst.rearrange("p (g c) -> p g c", g=4)
+                for lo, hi in cuts:
+                    src = W_words[g0 + lo:g0 + hi].rearrange("g p n t -> p g (n t)")[:, :, 4 * NA:4 * N].bitcast(I32)
+                    nc.sync.dma_start(out=dst3[:, lo:hi, :], in_=src)
+
+        for n in range(NW):
+            load_w(n)
+
+        vw = v_sb[:].bitcast(F32)
+        xts = []
+        for h in range(8):
+            xt = psum.tile([P, 2, 2, P], F32, name="xt%d" % h, tag="bank%d" % h)
+            xts.append(xt)
+            for gg in range(2):
+                g = 2 * h + gg
+                for u in range(2):
+                    nc.tensor.transpose(xt[:, gg, u, :], vw[:, 256 * g + u:256 * (g + 1):2], ident[:])
+
+        def copy_out(h):
+            dst = grouped[:, 2 * h:2 * h + 2, :, :]
+            src = xts[h][:].rearrange("p g u r -> p g r u")
+            if h % 2 == 0:
+                V.tensor_copy(out=dst, in_=src)
+            else:
+                A.copy(out=dst, in_=src)
+
+        def quant(i):
+            V.quantize_mx(
+                out=vcodes[:, 4 * i:4 * i + 4, :].rearrange("p g r -> p (g r)").bitcast(FP8X4),
+                scales=vscl[:, 4 * i:4 * i + 4, :].rearrange("p g r -> p (g r)"),
+                in_=grouped[:, 4 * i:4 * i + 4, :, :].rearrange("p g r u -> p (g r u)").bitcast(BF16),
+            )
+
+        copy_out(0)
+        copy_out(1)
+        copy_out(2)
+        copy_out(3)
+        quant(0)
+        copy_out(4)
+        copy_out(5)
+        quant(1)
+        copy_out(6)
+        copy_out(7)
+        quant(2)
+        quant(3)
+
+        for c in range(5):
+            pb = psum.tile([P, CH], F32, name="pb%d" % c, tag="bank%d" % (4 + c % 4))
+            nc.tensor.matmul(pb[:], lhsT=ones[:], rhs=bz[:, CH * c:CH * (c + 1)], start=True, stop=True)
+            A.copy(out=bbc[:, CH * c:CH * (c + 1)], in_=pb[:])
+
+        v2c = sm("v2c", 4)
+        for i in range(4):
+            A.activation(out=junk_a[:, 0:2048], in_=v_sb[:, 2048 * i:2048 * (i + 1)], func=ACTF.Square,
+                         accum_out=v2c[:, i:i + 1])
+        b2 = sm("b2")
+        A.activation(out=junk_a[:], in_=bbc[:], func=ACTF.Square, accum_out=b2[:])
+        z2 = sm("z2")
+        A.activation(out=junk_a[:], in_=z0[:], func=ACTF.Square, accum_out=z2[:])
+        zb = sm("zb")
+        stt(w[:], z0[:], 1.0, bbc[:], ALU.mult, ALU.mult, acc=zb[:])
+
+        v2 = sm("v2")
+        V.tensor_reduce(out=v2[:], in_=v2c[:], axis=AX.X, op=ALU.add)
+        v2m = sm("v2m")
+        ts(v2m[:], v2[:], EPS2, None, ALU.max)
+        rvn = sm("rvn")
+        nc.gpsimd.tensor_tensor(out=rvn[:], in0=v2m[:], in1=mh[:, 0:1], op=ALU.pow)
+        cl = sm("cl")
+        ts(cl[:], v2m[:], rvn[:], MAXN, ALU.mult, ALU.min)
+        onem = sm("onem")
+        ts(onem[:], cl[:], -1.0, 1.0, ALU.mult, ALU.add)
+        rom = sm("rom")
+        V.reciprocal(out=rom[:], in_=onem[:])
+        ratio = sm("ratio")
+        stt(ratio[:], cl[:], 1.0, rom[:], ALU.add, ALU.mult)
+        lnr = sm("lnr")
+        A.activation(out=lnr[:], in_=ratio[:], func=ACTF.Ln)
+        r = sm("r")
+        stt(r[:], lnr[:], 0.5, rvn[:], ALU.mult, ALU.mult)
+
+        b2m = sm("b2m")
+        ts(b2m[:], b2[:], EPS2, None, ALU.max)
+        rbn = sm("rbn")
+        nc.gpsimd.tensor_tensor(out=rbn[:], in0=b2m[:], in1=mh[:, 0:1], op=ALU.pow)
+        bn = sm("bn")
+        tt(bn[:], b2m[:], rbn[:], ALU.mult)
+        ths = sm("ths")
+        A.activation(out=ths[:], in_=ssb[:], func=ACTF.Tanh, scale=0.5)
+        tb = sm("tb")
+        A.activation(out=tb[:], in_=bn[:], func=ACTF.Tanh)
+        beta = sm("beta")
+        tt(beta[:], tb[:], rbn[:], ALU.mult)
+        beta2 = sm("beta2")
+        ts(beta2[:], beta[:], 2.0, None, ALU.mult)
+        y2 = sm("y2")
+        stt(y2[:], beta[:], beta[:], b2[:], ALU.mult, ALU.mult)
+        y2p1 = sm("y2p1")
+        ts(y2p1[:], y2[:], 1.0, None, ALU.add)
+        ny2 = sm("ny2")
+        ts(ny2[:], y2[:], -1.0, None, ALU.mult)
+        stept = sm("stept", 2)
+        ts(stept[:, 0:1], ths[:], 0.5, 0.5, ALU.mult, ALU.add)
+        ts(stept[:, 1:2], ths[:], 1.0, None, ALU.add)
+        qz = sm("qz")
+        ts(qz[:], z2[:], -1.0, 1.0, ALU.mult, ALU.add)
+        z2m1 = sm("z2m1")
+        ts(z2m1[:], z2[:], -1.0, None, ALU.add)
+        qzm = sm("qzm")
+        ts(qzm[:], qz[:], EPS, None, ALU.max)
+        hl = sm("hl")
+        V.reciprocal(out=hl[:], in_=qzm[:])
+
+        acc = []
+        for j in range(5):
+            at = psum.tile([P, CH], F32, name="acc%d" % j, tag="bank%d" % j)
+            acc.append(at)
+
+        def mx(g, j, wt, col):
+            k = 4 * (g % 4)
+            nc.tensor.matmul_mx(
+                out=acc[j][:],
+                lhsT=vcodes[:, g, :].bitcast(FP8X4),
+                lhsT_scale=vscl[:, g, :],
+                rhs=wt[:, col:col + CH].bitcast(FP8X4),
+                rhs_scale=planes[k:P, g // 4, CH * j:CH * (j + 1)],
+                start=(g == 0),
+                stop=(g == G - 1),
+            )
+
+        for n in range(G + 4):
+            if n < G:
+                for j in range(4):
+                    mx(n, j, wtiles[n], CH * j)
+            else:
+                for i in range(4):
+                    mx(4 * (n - G) + i, 4, wtiles[n], CH * i)
+            if n + NW < G + 4:
+                load_w(n + NW)
+            if n == G - 1:
+                sac = sm("sac", 4)
+                dac = sm("dac", 4)
+                zac = sm("zac", 4)
+                srun = [sm("srun%d" % j) for j in range(4)]
+                for j in range(4):
+                    cs = slice(CH * j, CH * (j + 1))
+                    A.activation(out=junk_a[:, 0:CH], in_=acc[j][:], func=ACTF.Square, accum_out=sac[:, j:j + 1])
+                    if j == 0:
+                        ts(srun[0][:], sac[:, 0:1], 0.0, None, ALU.add)
+                    else:
+                        tt(srun[j][:], srun[j - 1][:], sac[:, j:j + 1], ALU.add)
+                    stt(junk_v[:], acc[j][:], 1.0, bbc[:, cs], ALU.mult, ALU.mult, acc=dac[:, j:j + 1])
+                    stt(junk_v[:], acc[j][:], 1.0, z0[:, cs], ALU.mult, ALU.mult, acc=zac[:, j:j + 1])
+                sa = srun[3]
+                sap = sm("sap")
+                ts(sap[:], sa[:], EPS2, None, ALU.add)
+                da = sm("da")
+                V.tensor_reduce(out=da[:], in_=dac[:], axis=AX.X, op=ALU.add)
+                za = sm("za")
+                V.tensor_reduce(out=za[:], in_=zac[:], axis=AX.X, op=ALU.add)
+
+        csb = slice(NA, N)
+        sb = sm("sb")
+        A.activation(out=junk_a[:, 0:CH], in_=acc[4][:], func=ACTF.Square, accum_out=sb[:])
+        sx = sm("sx")
+        tt(sx[:], sb[:], sap[:], ALU.add)
+        rm = sm("rm")
+        nc.gpsimd.tensor_tensor(out=rm[:], in0=sx[:], in1=mh[:, 0:1], op=ALU.pow)
+        rs_ = sm("rs_")
+        tt(rs_[:], sx[:], r[:], ALU.mult)
+        st = sm("st")
+        tt(st[:], sb[:], sa[:], ALU.add)
+        db = sm("db")
+        stt(junk_v[:], acc[4][:], 1.0, bbc[:, csb], ALU.mult, ALU.mult, acc=db[:])
+        dp = sm("dp")
+        ts(dp[:], db[:], da[:], beta2[:], ALU.add, ALU.mult)
+        th = sm("th")
+        A.activation(out=th[:], in_=rm[:], func=ACTF.Tanh, scale=rs_[:])
+        s1 = sm("s1")
+        stt(s1[:], rm[:], rm[:], st[:], ALU.mult, ALU.mult)
+        al = sm("al")
+        tt(al[:], th[:], rm[:], ALU.mult)
+        x2 = sm("x2")
+        stt(x2[:], th[:], th[:], s1[:], ALU.mult, ALU.mult)
+        pp = sm("pp")
+        ts(pp[:], al[:], dp[:], y2p1[:], ALU.mult, ALU.add)
+        qq = sm("qq")
+        ts(qq[:], x2[:], -1.0, 1.0, ALU.mult, ALU.add)
+        e2 = sm("e2")
+        tt(e2[:], qq[:], beta[:], ALU.mult)
+        e1 = sm("e1")
+        tt(e1[:], pp[:], al[:], ALU.mult)
+
+        tmps = []
+
+        def make_tmp(c):
+            tm = tmpp.tile([P, CH], F32, name="tm%d" % c, tag="tm")
+            tmps.append(tm)
+            A.activation(out=tm[:], in_=bbc[:, CH * c:CH * (c + 1)], func=ACTF.Copy, scale=e2[:])
+
+        def make_w(c):
+            stt(w[:, CH * c:CH * (c + 1)], acc[c][:], e1[:], tmps[c][:], ALU.mult, ALU.add)
+
+        make_tmp(0)
+        make_tmp(1)
+        den0 = sm("den0")
+        stt(den0[:], qq[:], ny2[:], pp[:], ALU.mult, ALU.add)
+        n1 = sm("n1")
+        tt(n1[:], pp[:], qq[:], ALU.subtract)
+        ndm = sm("ndm")
+        stt(ndm[:], n1[:], den0[:], tiny[:], ALU.mult, ALU.max)
+        rs = sm("rs")
+        nc.gpsimd.tensor_tensor(out=rs[:], in0=ndm[:], in1=mh[:, 0:1], op=ALU.pow)
+        dmax = sm("dmax")
+        ts(dmax[:], den0[:], EPS, None, ALU.max)
+        rden = sm("rden")
+        V.reciprocal(out=rden[:], in_=dmax[:])
+        ndr = sm("ndr")
+        tt(ndr[:], ndm[:], rden[:], ALU.mult)
+        zbb = sm("zbb")
+        stt(junk_v[:], acc[4][:], 1.0, z0[:, csb], ALU.mult, ALU.mult, acc=zbb[:])
+        zz = sm("zz")
+        ts(zz[:], zbb[:], za[:], e1[:], ALU.add, ALU.mult)
+        zz2 = sm("zz2")
+        stt(zz2[:], e2[:], zb[:], zz[:], ALU.mult, ALU.add)
+        v0n = sm("v0n")
+        ts(v0n[:], rs[:], ndr[:], MAXN, ALU.mult, ALU.min)
+        vtn = sm("vtn", 2)
+        ts(vtn[:], stept[:], v0n[:], EPS, ALU.mult, ALU.max)
+        tht = sm("tht", 2)
+        A.activation(out=tht[:], in_=vtn[:], func=ACTF.Tanh, scale=hl[:])
+        make_tmp(2)
+        make_tmp(3)
+        make_tmp(4)
+        sc = sm("sc")
+        stt(sc[:], rs[:], MAXN, rden[:], ALU.mult, ALU.min)
+        rv = sm("rv", 2)
+        V.reciprocal(out=rv[:], in_=vtn[:])
+        qt = sm("qt", 2)
+        tt(qt[:], rv[:], stept[:], ALU.mult)
+        s2 = sm("s2", 2)
+        ts(s2[:], qt[:], v0n[:], None, ALU.mult)
+        zv2 = sm("zv2")
+        stt(zv2[:], zz2[:], 2.0, sc[:], ALU.mult, ALU.mult)
+        scq = sm("scq")
+        tt(scq[:], sc[:], qz[:], ALU.mult)
+        make_w(0)
+        gt = sm("gt", 2)
+        tt(gt[:], tht[:], qt[:], ALU.mult)
+        gv = sm("gv", 2)
+        tt(gv[:], tht[:], s2[:], ALU.mult)
+        y2t = sm("y2t", 2)
+        tt(y2t[:], gv[:], gv[:], ALU.mult)
+        base = sm("base", 2)
+        ts(base[:], gt[:], zv2[:], 1.0, ALU.mult, ALU.add)
+        den0t = sm("den0t", 2)
+        stt(den0t[:], y2t[:], z2[:], base[:], ALU.mult, ALU.add)
+        nt = sm("nt", 2)
+        stt(nt[:], base[:], z2m1[:], y2t[:], ALU.add, ALU.add)
+        ndt = sm("ndt", 2)
+        tt(ndt[:], nt[:], den0t[:], ALU.mult)
+        ndtm = sm("ndtm", 2)
+        ts(ndtm[:], ndt[:], TINY, None, ALU.max)
+        rst = sm("rst", 2)
+        nc.gpsimd.tensor_tensor(out=rst[:], in0=ndtm[:], in1=mh[:], op=ALU.pow)
+        dmt = sm("dmt", 2)
+        ts(dmt[:], den0t[:], EPS, None, ALU.max)
+        rdt = sm("rdt", 2)
+        V.reciprocal(out=rdt[:], in_=dmt[:])
+        pt = sm("pt", 2)
+        tt(pt[:], base[:], y2t[:], ALU.add)
+        gq = sm("gq", 2)
+        ts(gq[:], gt[:], scq[:], None, ALU.mult)
+        make_w(1)
+        sct = sm("sct", 2)
+        stt(sct[:], rst[:], MAXN, rdt[:], ALU.mult, ALU.min)
+        ca = sm("ca", 2)
+        tt(ca[:], sct[:], pt[:], ALU.mult)
+        cb = sm("cb", 2)
+        tt(cb[:], sct[:], gq[:], ALU.mult)
+
+        for c in range(5):
+            cs = slice(CH * c, CH * (c + 1))
+            if c >= 2:
+                make_w(c)
+            for t in range(2):
+                tz = tpool.tile([P, CH], F32, name="tz%d_%d" % (c, t), tag="tz")
+                A.activation(out=tz[:], in_=z0[:, cs], func=ACTF.Copy, scale=ca[:, t:t + 1])
+                ot = opool.tile([P, CH], F32, name="ot%d_%d" % (c, t), tag="ot")
+                stt(ot[:], w[:, cs], cb[:, t:t + 1], tz[:], ALU.mult, ALU.add)
+                nc.sync.dma_start(out=out[:, t, cs], in_=ot[:])

@@ -37,7 +37,6 @@ def tile_paralleldirectpoincaredynamics_w_kernel(tc, z_0, v_init, W_words, W_sca
         keep = ctx.enter_context(tc.tile_pool(name="keep", bufs=1))
         small = ctx.enter_context(tc.tile_pool(name="small", bufs=1))
         wpool = ctx.enter_context(tc.tile_pool(name="wpool", bufs=NW))
-        tmpp = ctx.enter_context(tc.tile_pool(name="tmpp", bufs=5))
         tpool = ctx.enter_context(tc.tile_pool(name="tpool", bufs=4))
         opool = ctx.enter_context(tc.tile_pool(name="opool", bufs=10))
         psum = ctx.enter_context(tc.psum_pool(name="psum", bufs=1))
@@ -63,11 +62,16 @@ def tile_paralleldirectpoincaredynamics_w_kernel(tc, z_0, v_init, W_words, W_sca
         vscl = keep.tile([P, G, P], U8, name="vscl", align_bytes=64)
         planes = keep.tile([P, 4, N], U8, name="planes", align_bytes=64)
         ident = keep.tile([P, P], F32, name="ident")
-        ones = keep.tile([P, P], BF16, name="ones")
-        bz = keep.tile([P, N], BF16, name="bz")
+        identb = keep.tile([P, P], BF16, name="identb")
+        sel = keep.tile([P, P], BF16, name="sel")
+        lp = keep.tile([P, P], BF16, name="lp")
+        lt = keep.tile([P, P], BF16, name="lt")
+        b2r = keep.tile([P, N], BF16, name="b2r")
         bbc = keep.tile([P, N], BF16, name="bbc")
         z0 = keep.tile([P, N], BF16, name="z0")
-        w = keep.tile([P, N], F32, name="w")
+        mhi = keep.tile([P, NA], BF16, name="mhi")
+        mmid = keep.tile([P, NA], BF16, name="mmid")
+        wb = keep.tile([P, CH], F32, name="wb")
         junk_a = keep.tile([P, N], BF16, name="junk_a")
         junk_v = keep.tile([P, CH], F32, name="junk_v")
         ssb = small.tile([P, 1], BF16, name="ssb")
@@ -77,13 +81,16 @@ def tile_paralleldirectpoincaredynamics_w_kernel(tc, z_0, v_init, W_words, W_sca
         for i in range(4):
             nc.sync.dma_start(out=v_sb[:, 2048 * i:2048 * (i + 1)], in_=v_init[:, 2048 * i:2048 * (i + 1)])
         V.memset(planes[:].rearrange("p j n -> p (j n)").bitcast(I32), 0)
-        V.memset(bz[:].bitcast(I32), 0)
-        V.memset(ones[:], 1.0)
+        V.memset(b2r[:].bitcast(I32), 0)
+        V.memset(sel[:], 0.0)
+        V.memset(sel[0:1, :], 1.0)
+        V.memset(lp[:], 0.0)
         V.memset(mh[:], -0.5)
         V.memset(tiny[:], TINY)
         make_identity(nc, ident[:])
+        make_identity(nc, identb[:])
         A.dma_start(out=ssb[:], in_=step_sizes.partition_broadcast(P))
-        A.dma_start(out=bz[0:1, :], in_=b.rearrange("(o n) -> o n", o=1))
+        A.dma_start(out=b2r[0:2, :], in_=b.partition_broadcast(2))
         for jj in range(4):
             for q in range(4):
                 nc.sync.dma_start(
@@ -152,7 +159,7 @@ def tile_paralleldirectpoincaredynamics_w_kernel(tc, z_0, v_init, W_words, W_sca
 
         for c in range(5):
             pb = psum.tile([P, CH], F32, name="pb%d" % c, tag="bank%d" % (4 + c % 4))
-            nc.tensor.matmul(pb[:], lhsT=ones[:], rhs=bz[:, CH * c:CH * (c + 1)], start=True, stop=True)
+            nc.tensor.matmul(pb[:], lhsT=sel[:], rhs=b2r[:, CH * c:CH * (c + 1)], start=True, stop=True)
             A.copy(out=bbc[:, CH * c:CH * (c + 1)], in_=pb[:])
 
         v2c = sm("v2c", 4)
@@ -163,8 +170,12 @@ def tile_paralleldirectpoincaredynamics_w_kernel(tc, z_0, v_init, W_words, W_sca
         A.activation(out=junk_a[:], in_=bbc[:], func=ACTF.Square, accum_out=b2[:])
         z2 = sm("z2")
         A.activation(out=junk_a[:], in_=z0[:], func=ACTF.Square, accum_out=z2[:])
+        zbc = sm("zbc", 5)
+        for c in range(5):
+            stt(junk_v[:], z0[:, CH * c:CH * (c + 1)], 1.0, bbc[:, CH * c:CH * (c + 1)], ALU.mult, ALU.mult,
+                acc=zbc[:, c:c + 1])
         zb = sm("zb")
-        stt(w[:], z0[:], 1.0, bbc[:], ALU.mult, ALU.mult, acc=zb[:])
+        V.tensor_reduce(out=zb[:], in_=zbc[:], axis=AX.X, op=ALU.add)
 
         v2 = sm("v2")
         V.tensor_reduce(out=v2[:], in_=v2c[:], axis=AX.X, op=ALU.add)
@@ -216,6 +227,10 @@ def tile_paralleldirectpoincaredynamics_w_kernel(tc, z_0, v_init, W_words, W_sca
         ts(qzm[:], qz[:], EPS, None, ALU.max)
         hl = sm("hl")
         V.reciprocal(out=hl[:], in_=qzm[:])
+        nbeta = sm("nbeta")
+        ts(nbeta[:], beta[:], -1.0, None, ALU.mult)
+        se = sm("se", 2)
+        ts(se[:], stept[:], 1.0 / EPS, None, ALU.mult)
 
         acc = []
         for j in range(5):
@@ -234,6 +249,18 @@ def tile_paralleldirectpoincaredynamics_w_kernel(tc, z_0, v_init, W_words, W_sca
                 stop=(g == G - 1),
             )
 
+        wps = []
+
+        def w_open(c):
+            wp = psum.tile([P, CH], F32, name="wp%d" % c, tag="bank%d" % c)
+            wps.append(wp)
+            cs = slice(CH * c, CH * (c + 1))
+            nc.tensor.matmul(wp[:], lhsT=identb[:], rhs=mhi[:, cs], start=True, stop=False)
+            nc.tensor.matmul(wp[:], lhsT=identb[:], rhs=mmid[:, cs], start=False, stop=False)
+
+        def w_close(c):
+            nc.tensor.matmul(wps[c][:], lhsT=lt[:], rhs=b2r[:, CH * c:CH * (c + 1)], start=False, stop=True)
+
         for n in range(G + 4):
             if n < G:
                 for j in range(4):
@@ -247,151 +274,164 @@ def tile_paralleldirectpoincaredynamics_w_kernel(tc, z_0, v_init, W_words, W_sca
                 sac = sm("sac", 4)
                 dac = sm("dac", 4)
                 zac = sm("zac", 4)
-                srun = [sm("srun%d" % j) for j in range(4)]
                 for j in range(4):
                     cs = slice(CH * j, CH * (j + 1))
                     A.activation(out=junk_a[:, 0:CH], in_=acc[j][:], func=ACTF.Square, accum_out=sac[:, j:j + 1])
-                    if j == 0:
-                        ts(srun[0][:], sac[:, 0:1], 0.0, None, ALU.add)
-                    else:
-                        tt(srun[j][:], srun[j - 1][:], sac[:, j:j + 1], ALU.add)
+                    A.copy(out=mhi[:, cs], in_=acc[j][:])
+                    stt(mmid[:, cs], mhi[:, cs], -1.0, acc[j][:], ALU.mult, ALU.add)
                     stt(junk_v[:], acc[j][:], 1.0, bbc[:, cs], ALU.mult, ALU.mult, acc=dac[:, j:j + 1])
                     stt(junk_v[:], acc[j][:], 1.0, z0[:, cs], ALU.mult, ALU.mult, acc=zac[:, j:j + 1])
-                sa = srun[3]
+                sa = sm("sa")
+                V.tensor_reduce(out=sa[:], in_=sac[:], axis=AX.X, op=ALU.add)
                 sap = sm("sap")
                 ts(sap[:], sa[:], EPS2, None, ALU.add)
                 da = sm("da")
                 V.tensor_reduce(out=da[:], in_=dac[:], axis=AX.X, op=ALU.add)
                 za = sm("za")
                 V.tensor_reduce(out=za[:], in_=zac[:], axis=AX.X, op=ALU.add)
+            if n >= G and n < G + 3:
+                w_open(n - G)
+        w_open(3)
 
+        GP = nc.gpsimd
         csb = slice(NA, N)
         sb = sm("sb")
         A.activation(out=junk_a[:, 0:CH], in_=acc[4][:], func=ACTF.Square, accum_out=sb[:])
         sx = sm("sx")
         tt(sx[:], sb[:], sap[:], ALU.add)
         rm = sm("rm")
-        nc.gpsimd.tensor_tensor(out=rm[:], in0=sx[:], in1=mh[:, 0:1], op=ALU.pow)
+        GP.tensor_tensor(out=rm[:], in0=sx[:], in1=mh[:, 0:1], op=ALU.pow)
         rs_ = sm("rs_")
-        tt(rs_[:], sx[:], r[:], ALU.mult)
-        st = sm("st")
-        tt(st[:], sb[:], sa[:], ALU.add)
-        db = sm("db")
-        stt(junk_v[:], acc[4][:], 1.0, bbc[:, csb], ALU.mult, ALU.mult, acc=db[:])
-        dp = sm("dp")
-        ts(dp[:], db[:], da[:], beta2[:], ALU.add, ALU.mult)
+        ts(rs_[:], sb[:], sap[:], r[:], ALU.add, ALU.mult)
         th = sm("th")
         A.activation(out=th[:], in_=rm[:], func=ACTF.Tanh, scale=rs_[:])
-        s1 = sm("s1")
-        stt(s1[:], rm[:], rm[:], st[:], ALU.mult, ALU.mult)
+        db = sm("db")
+        stt(junk_v[:], acc[4][:], 1.0, bbc[:, csb], ALU.mult, ALU.mult, acc=db[:])
+        d2 = sm("d2")
+        ts(d2[:], db[:], da[:], beta2[:], ALU.add, ALU.mult)
+        d2r = sm("d2r")
+        tt(d2r[:], d2[:], rm[:], ALU.mult)
+        a1 = sm("a1")
+        stt(a1[:], th[:], d2r[:], th[:], ALU.add, ALU.mult)
+        a2 = sm("a2")
+        stt(a2[:], th[:], y2[:], d2r[:], ALU.mult, ALU.add)
+        pp = sm("pp")
+        ts(pp[:], th[:], d2r[:], y2p1[:], ALU.mult, ALU.add)
         al = sm("al")
         tt(al[:], th[:], rm[:], ALU.mult)
         x2 = sm("x2")
-        stt(x2[:], th[:], th[:], s1[:], ALU.mult, ALU.mult)
-        pp = sm("pp")
-        ts(pp[:], al[:], dp[:], y2p1[:], ALU.mult, ALU.add)
-        qq = sm("qq")
-        ts(qq[:], x2[:], -1.0, 1.0, ALU.mult, ALU.add)
-        e2 = sm("e2")
-        tt(e2[:], qq[:], beta[:], ALU.mult)
+        tt(x2[:], th[:], th[:], ALU.mult)
+        n1 = sm("n1")
+        ts(n1[:], a1[:], y2[:], None, ALU.add)
+        den0 = sm("den0")
+        ts(den0[:], a2[:], th[:], 1.0, ALU.mult, ALU.add)
         e1 = sm("e1")
         tt(e1[:], pp[:], al[:], ALU.mult)
-
-        tmps = []
-
-        def make_tmp(c):
-            tm = tmpp.tile([P, CH], F32, name="tm%d" % c, tag="tm")
-            tmps.append(tm)
-            A.activation(out=tm[:], in_=bbc[:, CH * c:CH * (c + 1)], func=ACTF.Copy, scale=e2[:])
-
-        def make_w(c):
-            stt(w[:, CH * c:CH * (c + 1)], acc[c][:], e1[:], tmps[c][:], ALU.mult, ALU.add)
-
-        make_tmp(0)
-        make_tmp(1)
-        den0 = sm("den0")
-        stt(den0[:], qq[:], ny2[:], pp[:], ALU.mult, ALU.add)
-        n1 = sm("n1")
-        tt(n1[:], pp[:], qq[:], ALU.subtract)
+        e2 = sm("e2")
+        ts(e2[:], x2[:], nbeta[:], beta[:], ALU.mult, ALU.add)
         ndm = sm("ndm")
         stt(ndm[:], n1[:], den0[:], tiny[:], ALU.mult, ALU.max)
         rs = sm("rs")
-        nc.gpsimd.tensor_tensor(out=rs[:], in0=ndm[:], in1=mh[:, 0:1], op=ALU.pow)
+        GP.tensor_tensor(out=rs[:], in0=ndm[:], in1=mh[:, 0:1], op=ALU.pow)
         dmax = sm("dmax")
         ts(dmax[:], den0[:], EPS, None, ALU.max)
+        re1 = sm("re1")
+        V.reciprocal(out=re1[:], in_=e1[:])
+        zq = sm("zq")
+        tt(zq[:], e1[:], za[:], ALU.mult)
         rden = sm("rden")
         V.reciprocal(out=rden[:], in_=dmax[:])
+        rho = sm("rho")
+        tt(rho[:], e2[:], re1[:], ALU.mult)
+        tt(lp[:, 0:1], e2[:], re1[:], ALU.mult)
+        zp = sm("zp")
+        stt(zp[:], e2[:], zb[:], zq[:], ALU.mult, ALU.add)
         ndr = sm("ndr")
         tt(ndr[:], ndm[:], rden[:], ALU.mult)
+        tt(lp[:, 1:2], rho[:], lp[:, 0:1], ALU.subtract)
         zbb = sm("zbb")
         stt(junk_v[:], acc[4][:], 1.0, z0[:, csb], ALU.mult, ALU.mult, acc=zbb[:])
-        zz = sm("zz")
-        ts(zz[:], zbb[:], za[:], e1[:], ALU.add, ALU.mult)
-        zz2 = sm("zz2")
-        stt(zz2[:], e2[:], zb[:], zz[:], ALU.mult, ALU.add)
+        ltp = psum.tile([P, P], BF16, name="ltp", tag="bank5")
+        nc.tensor.transpose(ltp[:], lp[:], identb[:])
         v0n = sm("v0n")
         ts(v0n[:], rs[:], ndr[:], MAXN, ALU.mult, ALU.min)
+        rv0 = sm("rv0")
+        ts(rv0[:], rs[:], dmax[:], 1.0 / MAXN, ALU.mult, ALU.max)
+        zz2 = sm("zz2")
+        stt(zz2[:], zbb[:], e1[:], zp[:], ALU.mult, ALU.add)
+        sc = sm("sc")
+        stt(sc[:], rs[:], MAXN, rden[:], ALU.mult, ALU.min)
         vtn = sm("vtn", 2)
         ts(vtn[:], stept[:], v0n[:], EPS, ALU.mult, ALU.max)
         tht = sm("tht", 2)
         A.activation(out=tht[:], in_=vtn[:], func=ACTF.Tanh, scale=hl[:])
-        make_tmp(2)
-        make_tmp(3)
-        make_tmp(4)
-        sc = sm("sc")
-        stt(sc[:], rs[:], MAXN, rden[:], ALU.mult, ALU.min)
-        rv = sm("rv", 2)
-        V.reciprocal(out=rv[:], in_=vtn[:])
-        qt = sm("qt", 2)
-        tt(qt[:], rv[:], stept[:], ALU.mult)
+        A.copy(out=lt[:], in_=ltp[:])
+        for c in range(4):
+            w_close(c)
         s2 = sm("s2", 2)
-        ts(s2[:], qt[:], v0n[:], None, ALU.mult)
+        ts(s2[:], se[:], v0n[:], 1.0, ALU.mult, ALU.min)
+        qt = sm("qt", 2)
+        ts(qt[:], se[:], rv0[:], None, ALU.min)
         zv2 = sm("zv2")
         stt(zv2[:], zz2[:], 2.0, sc[:], ALU.mult, ALU.mult)
         scq = sm("scq")
         tt(scq[:], sc[:], qz[:], ALU.mult)
-        make_w(0)
-        gt = sm("gt", 2)
-        tt(gt[:], tht[:], qt[:], ALU.mult)
-        gv = sm("gv", 2)
-        tt(gv[:], tht[:], s2[:], ALU.mult)
-        y2t = sm("y2t", 2)
-        tt(y2t[:], gv[:], gv[:], ALU.mult)
-        base = sm("base", 2)
-        ts(base[:], gt[:], zv2[:], 1.0, ALU.mult, ALU.add)
-        den0t = sm("den0t", 2)
-        stt(den0t[:], y2t[:], z2[:], base[:], ALU.mult, ALU.add)
+        c2 = sm("c2", 2)
+        tt(c2[:], s2[:], s2[:], ALU.mult)
+        c1 = sm("c1", 2)
+        ts(c1[:], qt[:], zv2[:], None, ALU.mult)
+        sqe1 = sm("sqe1")
+        tt(sqe1[:], scq[:], e1[:], ALU.mult)
+        c2z = sm("c2z", 2)
+        ts(c2z[:], c2[:], z2[:], None, ALU.mult)
+        q1 = sm("q1", 2)
+        ts(q1[:], qt[:], sqe1[:], None, ALU.mult)
+        hh = sm("hh", 2)
+        hz = sm("hz", 2)
+        pt = sm("pt", 2)
         nt = sm("nt", 2)
-        stt(nt[:], base[:], z2m1[:], y2t[:], ALU.add, ALU.add)
-        ndt = sm("ndt", 2)
-        tt(ndt[:], nt[:], den0t[:], ALU.mult)
+        dnt = sm("dnt", 2)
         ndtm = sm("ndtm", 2)
-        ts(ndtm[:], ndt[:], TINY, None, ALU.max)
+        T2 = [slice(0, 1), slice(1, 2)]
+        for s in T2:
+            stt(hh[:, s], tht[:, s], c2[:, s], c1[:, s], ALU.mult, ALU.add)
+        g1 = sm("g1", 2)
+        tt(g1[:], tht[:], q1[:], ALU.mult)
+        for s in T2:
+            stt(hz[:, s], tht[:, s], c2z[:, s], c1[:, s], ALU.mult, ALU.add)
+        for s in T2:
+            ts(pt[:, s], hh[:, s], tht[:, s], 1.0, ALU.mult, ALU.add)
+        for s in T2:
+            ts(nt[:, s], hh[:, s], tht[:, s], z2[:], ALU.mult, ALU.add)
+        for s in T2:
+            ts(dnt[:, s], hz[:, s], tht[:, s], 1.0, ALU.mult, ALU.add)
+        rpt = sm("rpt", 2)
+        V.reciprocal(out=rpt[:], in_=pt[:])
+        for s in T2:
+            stt(ndtm[:, s], nt[:, s], dnt[:, s], tiny[:], ALU.mult, ALU.max)
         rst = sm("rst", 2)
         nc.gpsimd.tensor_tensor(out=rst[:], in0=ndtm[:], in1=mh[:], op=ALU.pow)
+        kt = sm("kt", 2)
+        tt(kt[:], g1[:], rpt[:], ALU.mult)
         dmt = sm("dmt", 2)
-        ts(dmt[:], den0t[:], EPS, None, ALU.max)
+        ts(dmt[:], dnt[:], EPS, None, ALU.max)
         rdt = sm("rdt", 2)
         V.reciprocal(out=rdt[:], in_=dmt[:])
-        pt = sm("pt", 2)
-        tt(pt[:], base[:], y2t[:], ALU.add)
-        gq = sm("gq", 2)
-        ts(gq[:], gt[:], scq[:], None, ALU.mult)
-        make_w(1)
         sct = sm("sct", 2)
-        stt(sct[:], rst[:], MAXN, rdt[:], ALU.mult, ALU.min)
         ca = sm("ca", 2)
-        tt(ca[:], sct[:], pt[:], ALU.mult)
-        cb = sm("cb", 2)
-        tt(cb[:], sct[:], gq[:], ALU.mult)
 
-        for c in range(5):
+        order = [(c, t) for c in range(5) for t in range(2)]
+        for i in range(10):
+            c, t = order[i]
             cs = slice(CH * c, CH * (c + 1))
-            if c >= 2:
-                make_w(c)
-            for t in range(2):
-                tz = tpool.tile([P, CH], F32, name="tz%d_%d" % (c, t), tag="tz")
-                A.activation(out=tz[:], in_=z0[:, cs], func=ACTF.Copy, scale=ca[:, t:t + 1])
-                ot = opool.tile([P, CH], F32, name="ot%d_%d" % (c, t), tag="ot")
-                stt(ot[:], w[:, cs], cb[:, t:t + 1], tz[:], ALU.mult, ALU.add)
-                nc.sync.dma_start(out=out[:, t, cs], in_=ot[:])
+            if i == 8:
+                stt(wb[:], bbc[:, csb], rho[:], acc[4][:], ALU.mult, ALU.add)
+            ut = tpool.tile([P, CH], F32, name="ut%d_%d" % (c, t), tag="ut")
+            src = wps[c][:] if c < 4 else wb[:]
+            stt(ut[:], src, kt[:, t:t + 1], z0[:, cs], ALU.mult, ALU.add)
+            if i == 0:
+                stt(sct[:], rst[:], MAXN, rdt[:], ALU.mult, ALU.min)
+                tt(ca[:], sct[:], pt[:], ALU.mult)
+            ot = opool.tile([P, CH], F32, name="ot%d_%d" % (c, t), tag="ot")
+            A.activation(out=ot[:], in_=ut[:], func=ACTF.Copy, scale=ca[:, t:t + 1])
+            nc.sync.dma_start(out=out[:, t, cs], in_=ot[:])

@@ -91,11 +91,12 @@ def tile_paralleldirectpoincaredynamics_w_kernel(tc, z_0, v_init, W_words, W_sca
         make_identity(nc, identb[:])
         A.dma_start(out=ssb[:], in_=step_sizes.partition_broadcast(P))
         A.dma_start(out=b2r[0:2, :], in_=b.partition_broadcast(2))
-        for jj in range(4):
-            for q in range(4):
-                nc.sync.dma_start(
-                    out=planes[32 * q:32 * q + 16, jj, :].bitcast(I32),
-                    in_=W_scales[4 * jj:4 * jj + 4, 4 * q:4 * q + 4, :].bitcast(I32),
+        wsv = W_scales.rearrange("(j k) q n -> k j q n", k=4)
+        for q in (0, 2, 1, 3):
+            for rr in range(4):
+                nc.gpsimd.dma_start(
+                    out=planes[32 * q + rr:32 * q + rr + 13:4, :, :].bitcast(F32),
+                    in_=wsv[:, :, 4 * q + rr, :].bitcast(F32),
                 )
         nc.sync.dma_start(out=z0[:], in_=z_0)
 
@@ -365,7 +366,7 @@ def tile_paralleldirectpoincaredynamics_w_kernel(tc, z_0, v_init, W_words, W_sca
         ts(vtn[:], stept[:], v0n[:], EPS, ALU.mult, ALU.max)
         tht = sm("tht", 2)
         A.activation(out=tht[:], in_=vtn[:], func=ACTF.Tanh, scale=hl[:])
-        A.copy(out=lt[:], in_=ltp[:])
+        V.tensor_copy(out=lt[:], in_=ltp[:])
         for c in range(4):
             w_close(c)
         s2 = sm("s2", 2)
@@ -388,6 +389,7 @@ def tile_paralleldirectpoincaredynamics_w_kernel(tc, z_0, v_init, W_words, W_sca
         ts(q1[:], qt[:], sqe1[:], None, ALU.mult)
         hh = sm("hh", 2)
         hz = sm("hz", 2)
+        g1 = sm("g1", 2)
         pt = sm("pt", 2)
         nt = sm("nt", 2)
         dnt = sm("dnt", 2)
@@ -395,24 +397,24 @@ def tile_paralleldirectpoincaredynamics_w_kernel(tc, z_0, v_init, W_words, W_sca
         T2 = [slice(0, 1), slice(1, 2)]
         for s in T2:
             stt(hh[:, s], tht[:, s], c2[:, s], c1[:, s], ALU.mult, ALU.add)
-        g1 = sm("g1", 2)
-        tt(g1[:], tht[:], q1[:], ALU.mult)
+        for s in T2:
+            ts(g1[:, s], tht[:, s], q1[:, s], TINY, ALU.mult, ALU.add)
         for s in T2:
             stt(hz[:, s], tht[:, s], c2z[:, s], c1[:, s], ALU.mult, ALU.add)
         for s in T2:
             ts(pt[:, s], hh[:, s], tht[:, s], 1.0, ALU.mult, ALU.add)
+        rg = sm("rg", 2)
+        V.reciprocal(out=rg[:], in_=g1[:])
         for s in T2:
             ts(nt[:, s], hh[:, s], tht[:, s], z2[:], ALU.mult, ALU.add)
         for s in T2:
             ts(dnt[:, s], hz[:, s], tht[:, s], 1.0, ALU.mult, ALU.add)
-        rpt = sm("rpt", 2)
-        V.reciprocal(out=rpt[:], in_=pt[:])
+        jt = sm("jt", 2)
+        tt(jt[:], pt[:], rg[:], ALU.mult)
         for s in T2:
             stt(ndtm[:, s], nt[:, s], dnt[:, s], tiny[:], ALU.mult, ALU.max)
         rst = sm("rst", 2)
-        nc.gpsimd.tensor_tensor(out=rst[:], in0=ndtm[:], in1=mh[:], op=ALU.pow)
-        kt = sm("kt", 2)
-        tt(kt[:], g1[:], rpt[:], ALU.mult)
+        GP.tensor_tensor(out=rst[:], in0=ndtm[:], in1=mh[:], op=ALU.pow)
         dmt = sm("dmt", 2)
         ts(dmt[:], dnt[:], EPS, None, ALU.max)
         rdt = sm("rdt", 2)
@@ -428,10 +430,10 @@ def tile_paralleldirectpoincaredynamics_w_kernel(tc, z_0, v_init, W_words, W_sca
                 stt(wb[:], bbc[:, csb], rho[:], acc[4][:], ALU.mult, ALU.add)
             ut = tpool.tile([P, CH], F32, name="ut%d_%d" % (c, t), tag="ut")
             src = wps[c][:] if c < 4 else wb[:]
-            stt(ut[:], src, kt[:, t:t + 1], z0[:, cs], ALU.mult, ALU.add)
+            stt(ut[:], z0[:, cs], jt[:, t:t + 1], src, ALU.mult, ALU.add)
             if i == 0:
                 stt(sct[:], rst[:], MAXN, rdt[:], ALU.mult, ALU.min)
-                tt(ca[:], sct[:], pt[:], ALU.mult)
+                tt(ca[:], sct[:], g1[:], ALU.mult)
             ot = opool.tile([P, CH], F32, name="ot%d_%d" % (c, t), tag="ot")
             A.activation(out=ot[:], in_=ut[:], func=ACTF.Copy, scale=ca[:, t:t + 1])
             nc.sync.dma_start(out=out[:, t, cs], in_=ot[:])

@@ -69,8 +69,7 @@ def tile_paralleldirectpoincaredynamics_w_kernel(tc, z_0, v_init, W_words, W_sca
         b2r = keep.tile([P, N], BF16, name="b2r")
         bbc = keep.tile([P, N], BF16, name="bbc")
         z0 = keep.tile([P, N], BF16, name="z0")
-        mhi = keep.tile([P, NA], BF16, name="mhi")
-        mmid = keep.tile([P, NA], BF16, name="mmid")
+        mv = keep.tile([P, NA], F32, name="mv")
         wb = keep.tile([P, CH], F32, name="wb")
         junk_a = keep.tile([P, N], BF16, name="junk_a")
         junk_v = keep.tile([P, CH], F32, name="junk_v")
@@ -91,12 +90,11 @@ def tile_paralleldirectpoincaredynamics_w_kernel(tc, z_0, v_init, W_words, W_sca
         make_identity(nc, identb[:])
         A.dma_start(out=ssb[:], in_=step_sizes.partition_broadcast(P))
         A.dma_start(out=b2r[0:2, :], in_=b.partition_broadcast(2))
-        wsv = W_scales.rearrange("(j k) q n -> k j q n", k=4)
-        for q in (0, 2, 1, 3):
-            for rr in range(4):
-                nc.gpsimd.dma_start(
-                    out=planes[32 * q + rr:32 * q + rr + 13:4, :, :].bitcast(F32),
-                    in_=wsv[:, :, 4 * q + rr, :].bitcast(F32),
+        for jj in range(4):
+            for q in range(4):
+                nc.sync.dma_start(
+                    out=planes[32 * q:32 * q + 16, jj, :].bitcast(I32),
+                    in_=W_scales[4 * jj:4 * jj + 4, 4 * q:4 * q + 4, :].bitcast(I32),
                 )
         nc.sync.dma_start(out=z0[:], in_=z_0)
 
@@ -213,25 +211,33 @@ def tile_paralleldirectpoincaredynamics_w_kernel(tc, z_0, v_init, W_words, W_sca
         ts(beta2[:], beta[:], 2.0, None, ALU.mult)
         y2 = sm("y2")
         stt(y2[:], beta[:], beta[:], b2[:], ALU.mult, ALU.mult)
-        y2p1 = sm("y2p1")
-        ts(y2p1[:], y2[:], 1.0, None, ALU.add)
-        ny2 = sm("ny2")
-        ts(ny2[:], y2[:], -1.0, None, ALU.mult)
         stept = sm("stept", 2)
         ts(stept[:, 0:1], ths[:], 0.5, 0.5, ALU.mult, ALU.add)
         ts(stept[:, 1:2], ths[:], 1.0, None, ALU.add)
         qz = sm("qz")
         ts(qz[:], z2[:], -1.0, 1.0, ALU.mult, ALU.add)
-        z2m1 = sm("z2m1")
-        ts(z2m1[:], z2[:], -1.0, None, ALU.add)
         qzm = sm("qzm")
         ts(qzm[:], qz[:], EPS, None, ALU.max)
         hl = sm("hl")
         V.reciprocal(out=hl[:], in_=qzm[:])
-        nbeta = sm("nbeta")
-        ts(nbeta[:], beta[:], -1.0, None, ALU.mult)
         se = sm("se", 2)
         ts(se[:], stept[:], 1.0 / EPS, None, ALU.mult)
+        xq1 = small.tile([P, 3, 3], F32, name="xq1")
+        cq1 = small.tile([P, 3, 3], F32, name="cq1")
+        oq1 = small.tile([P, 3, 3], F32, name="oq1")
+        xq2 = small.tile([P, 2, 3, 3], F32, name="xq2")
+        cq2 = small.tile([P, 2, 3, 3], F32, name="cq2")
+        oq2 = small.tile([P, 2, 3, 3], F32, name="oq2")
+        V.memset(xq1[:], 0.0)
+        V.memset(xq2[:], 0.0)
+        V.memset(cq1[:], 0.0)
+        V.memset(cq1[:, 0, 0:1], 1.0)
+        V.memset(cq1[:, 1, 2:3], 1.0)
+        ts(cq1[:, 1, 0:1], y2[:], 0.0, None, ALU.add)
+        ts(cq1[:, 0, 2:3], y2[:], 0.0, None, ALU.add)
+        ts(cq1[:, 2, 2:3], y2[:], 1.0, None, ALU.add)
+        V.memset(cq2[:], 1.0)
+        ts(cq2[:, :, 1, 2], z2[:].to_broadcast([P, 2]), 0.0, None, ALU.add)
 
         acc = []
         for j in range(5):
@@ -256,8 +262,7 @@ def tile_paralleldirectpoincaredynamics_w_kernel(tc, z_0, v_init, W_words, W_sca
             wp = psum.tile([P, CH], F32, name="wp%d" % c, tag="bank%d" % c)
             wps.append(wp)
             cs = slice(CH * c, CH * (c + 1))
-            nc.tensor.matmul(wp[:], lhsT=identb[:], rhs=mhi[:, cs], start=True, stop=False)
-            nc.tensor.matmul(wp[:], lhsT=identb[:], rhs=mmid[:, cs], start=False, stop=False)
+            nc.tensor.matmul(wp[:], lhsT=ident[:], rhs=mv[:, cs], start=True, stop=False)
 
         def w_close(c):
             nc.tensor.matmul(wps[c][:], lhsT=lt[:], rhs=b2r[:, CH * c:CH * (c + 1)], start=False, stop=True)
@@ -277,11 +282,10 @@ def tile_paralleldirectpoincaredynamics_w_kernel(tc, z_0, v_init, W_words, W_sca
                 zac = sm("zac", 4)
                 for j in range(4):
                     cs = slice(CH * j, CH * (j + 1))
+                    A.copy(out=mv[:, cs], in_=acc[j][:])
                     A.activation(out=junk_a[:, 0:CH], in_=acc[j][:], func=ACTF.Square, accum_out=sac[:, j:j + 1])
-                    A.copy(out=mhi[:, cs], in_=acc[j][:])
-                    stt(mmid[:, cs], mhi[:, cs], -1.0, acc[j][:], ALU.mult, ALU.add)
-                    stt(junk_v[:], acc[j][:], 1.0, bbc[:, cs], ALU.mult, ALU.mult, acc=dac[:, j:j + 1])
-                    stt(junk_v[:], acc[j][:], 1.0, z0[:, cs], ALU.mult, ALU.mult, acc=zac[:, j:j + 1])
+                    stt(junk_v[:], mv[:, cs], 1.0, bbc[:, cs], ALU.mult, ALU.mult, acc=dac[:, j:j + 1])
+                    stt(junk_v[:], mv[:, cs], 1.0, z0[:, cs], ALU.mult, ALU.mult, acc=zac[:, j:j + 1])
                 sa = sm("sa")
                 V.tensor_reduce(out=sa[:], in_=sac[:], axis=AX.X, op=ALU.add)
                 sap = sm("sap")
@@ -290,9 +294,8 @@ def tile_paralleldirectpoincaredynamics_w_kernel(tc, z_0, v_init, W_words, W_sca
                 V.tensor_reduce(out=da[:], in_=dac[:], axis=AX.X, op=ALU.add)
                 za = sm("za")
                 V.tensor_reduce(out=za[:], in_=zac[:], axis=AX.X, op=ALU.add)
-            if n >= G and n < G + 3:
-                w_open(n - G)
-        w_open(3)
+        for c in range(4):
+            w_open(c)
 
         GP = nc.gpsimd
         csb = slice(NA, N)
@@ -304,51 +307,51 @@ def tile_paralleldirectpoincaredynamics_w_kernel(tc, z_0, v_init, W_words, W_sca
         GP.tensor_tensor(out=rm[:], in0=sx[:], in1=mh[:, 0:1], op=ALU.pow)
         rs_ = sm("rs_")
         ts(rs_[:], sb[:], sap[:], r[:], ALU.add, ALU.mult)
-        th = sm("th")
-        A.activation(out=th[:], in_=rm[:], func=ACTF.Tanh, scale=rs_[:])
+        A.activation(out=xq1[:, :, 1:3], in_=rm[:].unsqueeze(2).to_broadcast([P, 3, 2]), func=ACTF.Tanh, scale=rs_[:])
+        th = xq1[:, 0, 1:2]
         db = sm("db")
         stt(junk_v[:], acc[4][:], 1.0, bbc[:, csb], ALU.mult, ALU.mult, acc=db[:])
         d2 = sm("d2")
         ts(d2[:], db[:], da[:], beta2[:], ALU.add, ALU.mult)
-        d2r = sm("d2r")
-        tt(d2r[:], d2[:], rm[:], ALU.mult)
-        a1 = sm("a1")
-        stt(a1[:], th[:], d2r[:], th[:], ALU.add, ALU.mult)
-        a2 = sm("a2")
-        stt(a2[:], th[:], y2[:], d2r[:], ALU.mult, ALU.add)
-        pp = sm("pp")
-        ts(pp[:], th[:], d2r[:], y2p1[:], ALU.mult, ALU.add)
-        al = sm("al")
-        tt(al[:], th[:], rm[:], ALU.mult)
-        x2 = sm("x2")
-        tt(x2[:], th[:], th[:], ALU.mult)
-        n1 = sm("n1")
-        ts(n1[:], a1[:], y2[:], None, ALU.add)
-        den0 = sm("den0")
-        ts(den0[:], a2[:], th[:], 1.0, ALU.mult, ALU.add)
-        e1 = sm("e1")
-        tt(e1[:], pp[:], al[:], ALU.mult)
-        e2 = sm("e2")
-        ts(e2[:], x2[:], nbeta[:], beta[:], ALU.mult, ALU.add)
+        ts(cq1[:, :, 1], d2[:].to_broadcast([P, 3]), rm[:], None, ALU.mult)
+        V.tensor_tensor_scan(
+            out=oq1[:].rearrange("p g e -> p (g e)"),
+            data0=xq1[:].rearrange("p g e -> p (g e)"),
+            data1=cq1[:].rearrange("p g e -> p (g e)"),
+            initial=0.0, op0=ALU.mult, op1=ALU.add,
+        )
+        n1 = oq1[:, 0, 2:3]
+        den0 = oq1[:, 1, 2:3]
+        pp = oq1[:, 2, 2:3]
         ndm = sm("ndm")
-        stt(ndm[:], n1[:], den0[:], tiny[:], ALU.mult, ALU.max)
+        stt(ndm[:], n1, den0, tiny[:], ALU.mult, ALU.max)
         rs = sm("rs")
         GP.tensor_tensor(out=rs[:], in0=ndm[:], in1=mh[:, 0:1], op=ALU.pow)
         dmax = sm("dmax")
-        ts(dmax[:], den0[:], EPS, None, ALU.max)
+        ts(dmax[:], den0, EPS, None, ALU.max)
+        al = sm("al")
+        tt(al[:], th, rm[:], ALU.mult)
+        qq = sm("qq")
+        tt(qq[:], pp, n1, ALU.subtract)
+        rden = sm("rden")
+        V.reciprocal(out=rden[:], in_=dmax[:])
+        e1 = sm("e1")
+        tt(e1[:], pp, al[:], ALU.mult)
+        e2 = sm("e2")
+        tt(e2[:], qq[:], beta[:], ALU.mult)
+        ndr = sm("ndr")
+        tt(ndr[:], ndm[:], rden[:], ALU.mult)
         re1 = sm("re1")
         V.reciprocal(out=re1[:], in_=e1[:])
         zq = sm("zq")
         tt(zq[:], e1[:], za[:], ALU.mult)
-        rden = sm("rden")
-        V.reciprocal(out=rden[:], in_=dmax[:])
+        qe = sm("qe")
+        tt(qe[:], e1[:], qz[:], ALU.mult)
         rho = sm("rho")
         tt(rho[:], e2[:], re1[:], ALU.mult)
         tt(lp[:, 0:1], e2[:], re1[:], ALU.mult)
         zp = sm("zp")
         stt(zp[:], e2[:], zb[:], zq[:], ALU.mult, ALU.add)
-        ndr = sm("ndr")
-        tt(ndr[:], ndm[:], rden[:], ALU.mult)
         tt(lp[:, 1:2], rho[:], lp[:, 0:1], ALU.subtract)
         zbb = sm("zbb")
         stt(junk_v[:], acc[4][:], 1.0, z0[:, csb], ALU.mult, ALU.mult, acc=zbb[:])
@@ -358,65 +361,54 @@ def tile_paralleldirectpoincaredynamics_w_kernel(tc, z_0, v_init, W_words, W_sca
         ts(v0n[:], rs[:], ndr[:], MAXN, ALU.mult, ALU.min)
         rv0 = sm("rv0")
         ts(rv0[:], rs[:], dmax[:], 1.0 / MAXN, ALU.mult, ALU.max)
-        zz2 = sm("zz2")
-        stt(zz2[:], zbb[:], e1[:], zp[:], ALU.mult, ALU.add)
         sc = sm("sc")
         stt(sc[:], rs[:], MAXN, rden[:], ALU.mult, ALU.min)
+        zz2 = sm("zz2")
+        stt(zz2[:], zbb[:], e1[:], zp[:], ALU.mult, ALU.add)
         vtn = sm("vtn", 2)
         ts(vtn[:], stept[:], v0n[:], EPS, ALU.mult, ALU.max)
-        tht = sm("tht", 2)
-        A.activation(out=tht[:], in_=vtn[:], func=ACTF.Tanh, scale=hl[:])
-        V.tensor_copy(out=lt[:], in_=ltp[:])
-        for c in range(4):
-            w_close(c)
+        A.activation(out=xq2[:, :, :, 1:3], in_=vtn[:].unsqueeze(2).unsqueeze(3).to_broadcast([P, 2, 3, 2]),
+                     func=ACTF.Tanh, scale=hl[:])
+        tht = xq2[:, :, 0, 1]
         s2 = sm("s2", 2)
         ts(s2[:], se[:], v0n[:], 1.0, ALU.mult, ALU.min)
         qt = sm("qt", 2)
         ts(qt[:], se[:], rv0[:], None, ALU.min)
         zv2 = sm("zv2")
         stt(zv2[:], zz2[:], 2.0, sc[:], ALU.mult, ALU.mult)
-        scq = sm("scq")
-        tt(scq[:], sc[:], qz[:], ALU.mult)
-        c2 = sm("c2", 2)
-        tt(c2[:], s2[:], s2[:], ALU.mult)
-        c1 = sm("c1", 2)
-        ts(c1[:], qt[:], zv2[:], None, ALU.mult)
         sqe1 = sm("sqe1")
-        tt(sqe1[:], scq[:], e1[:], ALU.mult)
-        c2z = sm("c2z", 2)
-        ts(c2z[:], c2[:], z2[:], None, ALU.mult)
+        tt(sqe1[:], sc[:], qe[:], ALU.mult)
+        s2b = s2[:].unsqueeze(2).to_broadcast([P, 2, 2])
+        tt(cq2[:, :, 0:2, 0], s2b, s2b, ALU.mult)
+        stt(cq2[:, :, 2, 0], s2[:], z2[:], s2[:], ALU.mult, ALU.mult)
+        ts(cq2[:, :, :, 1], qt[:].unsqueeze(2).to_broadcast([P, 2, 3]), zv2[:], None, ALU.mult)
         q1 = sm("q1", 2)
-        ts(q1[:], qt[:], sqe1[:], None, ALU.mult)
-        hh = sm("hh", 2)
-        hz = sm("hz", 2)
-        g1 = sm("g1", 2)
-        pt = sm("pt", 2)
-        nt = sm("nt", 2)
-        dnt = sm("dnt", 2)
-        ndtm = sm("ndtm", 2)
-        T2 = [slice(0, 1), slice(1, 2)]
-        for s in T2:
-            stt(hh[:, s], tht[:, s], c2[:, s], c1[:, s], ALU.mult, ALU.add)
-        for s in T2:
-            ts(g1[:, s], tht[:, s], q1[:, s], TINY, ALU.mult, ALU.add)
-        for s in T2:
-            stt(hz[:, s], tht[:, s], c2z[:, s], c1[:, s], ALU.mult, ALU.add)
-        for s in T2:
-            ts(pt[:, s], hh[:, s], tht[:, s], 1.0, ALU.mult, ALU.add)
-        rg = sm("rg", 2)
-        V.reciprocal(out=rg[:], in_=g1[:])
-        for s in T2:
-            ts(nt[:, s], hh[:, s], tht[:, s], z2[:], ALU.mult, ALU.add)
-        for s in T2:
-            ts(dnt[:, s], hz[:, s], tht[:, s], 1.0, ALU.mult, ALU.add)
+        ts(q1[:], qt[:], sqe1[:], TINY, ALU.mult, ALU.add)
+        rq1 = sm("rq1", 2)
+        V.reciprocal(out=rq1[:], in_=q1[:])
+        V.tensor_copy(out=lt[:], in_=ltp[:])
+        for c in range(4):
+            w_close(c)
+        V.tensor_tensor_scan(
+            out=oq2[:].rearrange("p t g e -> p (t g e)"),
+            data0=xq2[:].rearrange("p t g e -> p (t g e)"),
+            data1=cq2[:].rearrange("p t g e -> p (t g e)"),
+            initial=0.0, op0=ALU.mult, op1=ALU.add,
+        )
+        rt = sm("rt", 2)
+        V.reciprocal(out=rt[:], in_=tht)
         jt = sm("jt", 2)
-        tt(jt[:], pt[:], rg[:], ALU.mult)
-        for s in T2:
-            stt(ndtm[:, s], nt[:, s], dnt[:, s], tiny[:], ALU.mult, ALU.max)
+        ndtm = sm("ndtm", 2)
+        for t in range(2):
+            stt(jt[:, t:t + 1], oq2[:, t, 0, 2:3], rt[:, t:t + 1], rq1[:, t:t + 1], ALU.mult, ALU.mult)
+        for t in range(2):
+            stt(ndtm[:, t:t + 1], oq2[:, t, 1, 2:3], oq2[:, t, 2, 2:3], tiny[:], ALU.mult, ALU.max)
         rst = sm("rst", 2)
         GP.tensor_tensor(out=rst[:], in0=ndtm[:], in1=mh[:], op=ALU.pow)
         dmt = sm("dmt", 2)
-        ts(dmt[:], dnt[:], EPS, None, ALU.max)
+        ts(dmt[:], oq2[:, :, 2, 2], EPS, None, ALU.max)
+        g1 = sm("g1", 2)
+        tt(g1[:], tht, q1[:], ALU.mult)
         rdt = sm("rdt", 2)
         V.reciprocal(out=rdt[:], in_=dmt[:])
         sct = sm("sct", 2)

@@ -10,422 +10,423 @@ U32 = mybir.dt.uint32
 U8 = mybir.dt.uint8
 FP8X4 = mybir.dt.float8_e4m3fn_x4
 ALU = mybir.AluOpType
-ACTF = mybir.ActivationFunctionType
+ACT = mybir.ActivationFunctionType
 AX = mybir.AxisListType
 
 P = 128
 K = 8192
 N = 2560
-G = 16
-CH = 512
-NA = 2048
-NW = 12
+PASSES = K // 512
+BANK = 512
+N_FIRST = 2048
+CHUNKS = N // BANK
+LAST = CHUNKS - 1
+W_TILES = PASSES + PASSES // 4
+W_BUFS = 12
 EPS = 1e-7
-EPS2 = 1e-14
+EPS_SQ = 1e-14
+MAX_NORM = 1.0 - 1e-5
 TINY = 1e-30
-MAXN = 1.0 - 1e-5
 
 FLOPS = 2 * P * K * N
 
 
 def tile_paralleldirectpoincaredynamics_w_kernel(tc, z_0, v_init, W_words, W_scales, b, step_sizes, out):
     nc = tc.nc
-    V = nc.vector
-    A = nc.scalar
     with ExitStack() as ctx:
         ctx.enter_context(tc.manual_schedule())
         keep = ctx.enter_context(tc.tile_pool(name="keep", bufs=1))
-        small = ctx.enter_context(tc.tile_pool(name="small", bufs=1))
-        wpool = ctx.enter_context(tc.tile_pool(name="wpool", bufs=NW))
-        tpool = ctx.enter_context(tc.tile_pool(name="tpool", bufs=4))
-        opool = ctx.enter_context(tc.tile_pool(name="opool", bufs=10))
+        rows = ctx.enter_context(tc.tile_pool(name="rows", bufs=1))
+        weights = ctx.enter_context(tc.tile_pool(name="weights", bufs=W_BUFS))
+        unscaled = ctx.enter_context(tc.tile_pool(name="unscaled", bufs=4))
+        scaled = ctx.enter_context(tc.tile_pool(name="scaled", bufs=2 * CHUNKS))
         psum = ctx.enter_context(tc.psum_pool(name="psum", bufs=1))
 
-        def sm(name, cols=1):
-            return small.tile([P, cols], F32, name=name)
+        def row_value(name, cols=1):
+            return rows.tile([P, cols], F32, name=name)
 
-        def ts(o, i, s1, s2, op0, op1=None):
+        def scal(o, i, s1, op0, s2=None, op1=None):
             if op1 is None:
-                V.tensor_scalar(out=o, in0=i, scalar1=s1, scalar2=None, op0=op0)
+                nc.vector.tensor_scalar(out=o, in0=i, scalar1=s1, scalar2=None, op0=op0)
             else:
-                V.tensor_scalar(out=o, in0=i, scalar1=s1, scalar2=s2, op0=op0, op1=op1)
+                nc.vector.tensor_scalar(out=o, in0=i, scalar1=s1, scalar2=s2, op0=op0, op1=op1)
 
-        def stt(o, i0, s, i1, op0, op1, acc=None):
-            V.scalar_tensor_tensor(out=o, in0=i0, scalar=s, in1=i1, op0=op0, op1=op1, accum_out=acc)
+        def fused(o, i0, op0, s, op1, i1, total=None):
+            nc.vector.scalar_tensor_tensor(out=o, in0=i0, scalar=s, in1=i1, op0=op0, op1=op1, accum_out=total)
 
-        def tt(o, i0, i1, op):
-            V.tensor_tensor(out=o, in0=i0, in1=i1, op=op)
+        def pair(o, i0, op, i1):
+            nc.vector.tensor_tensor(out=o, in0=i0, in1=i1, op=op)
+
+        def inverse(o, i):
+            nc.vector.reciprocal(out=o, in_=i)
+
+        def inverse_root(o, i, cols=1):
+            nc.gpsimd.tensor_tensor(out=o, in0=i, in1=minus_half[:, 0:cols], op=ALU.pow)
+
+        def horner(o, x, abc):
+            nc.vector.tensor_tensor_scan(out=o, data0=x, data1=abc, initial=0.0, op0=ALU.mult, op1=ALU.add)
+
+        def chunk(c):
+            return slice(BANK * c, BANK * (c + 1))
 
         v_sb = keep.tile([P, K], BF16, name="v_sb", align_bytes=64)
-        grouped = keep.tile([P, G, P, 2], F32, name="grouped", align_bytes=64)
-        vcodes = keep.tile([P, G, P], U32, name="vcodes", align_bytes=64)
-        vscl = keep.tile([P, G, P], U8, name="vscl", align_bytes=64)
-        planes = keep.tile([P, 4, N], U8, name="planes", align_bytes=64)
-        ident = keep.tile([P, P], F32, name="ident")
-        identb = keep.tile([P, P], BF16, name="identb")
-        sel = keep.tile([P, P], BF16, name="sel")
-        lp = keep.tile([P, P], BF16, name="lp")
-        lt = keep.tile([P, P], BF16, name="lt")
-        b2r = keep.tile([P, N], BF16, name="b2r")
-        bbc = keep.tile([P, N], BF16, name="bbc")
-        z0 = keep.tile([P, N], BF16, name="z0")
-        mv = keep.tile([P, NA], F32, name="mv")
-        wb = keep.tile([P, CH], F32, name="wb")
-        junk_a = keep.tile([P, N], BF16, name="junk_a")
-        junk_v = keep.tile([P, CH], F32, name="junk_v")
-        ssb = small.tile([P, 1], BF16, name="ssb")
-        mh = sm("mh", 2)
-        tiny = sm("tiny", 1)
+        v_words = keep.tile([P, PASSES, P, 2], F32, name="v_words", align_bytes=64)
+        v_codes = keep.tile([P, PASSES, P], U32, name="v_codes", align_bytes=64)
+        v_scales = keep.tile([P, PASSES, P], U8, name="v_scales", align_bytes=64)
+        w_planes = keep.tile([P, PASSES // 4, N], U8, name="w_planes", align_bytes=64)
+        ident_f32 = keep.tile([P, P], F32, name="ident_f32")
+        ident_bf16 = keep.tile([P, P], BF16, name="ident_bf16")
+        first_row = keep.tile([P, P], BF16, name="first_row")
+        rho_cols = keep.tile([P, P], BF16, name="rho_cols")
+        rho_rows = keep.tile([P, P], BF16, name="rho_rows")
+        b_rows = keep.tile([P, N], BF16, name="b_rows")
+        b_all = keep.tile([P, N], BF16, name="b_all")
+        z_sb = keep.tile([P, N], BF16, name="z_sb")
+        mv_first = keep.tile([P, N_FIRST], F32, name="mv_first")
+        w_last = keep.tile([P, BANK], F32, name="w_last")
+        scrap_s = keep.tile([P, N], BF16, name="scrap_s")
+        scrap_v = keep.tile([P, BANK], F32, name="scrap_v")
+        step_logit = rows.tile([P, 1], BF16, name="step_logit")
+        minus_half = row_value("minus_half", 2)
+        tiny = row_value("tiny")
 
         for i in range(4):
-            nc.sync.dma_start(out=v_sb[:, 2048 * i:2048 * (i + 1)], in_=v_init[:, 2048 * i:2048 * (i + 1)])
-        V.memset(planes[:].rearrange("p j n -> p (j n)").bitcast(I32), 0)
-        V.memset(b2r[:].bitcast(I32), 0)
-        V.memset(sel[:], 0.0)
-        V.memset(sel[0:1, :], 1.0)
-        V.memset(lp[:], 0.0)
-        V.memset(mh[:], -0.5)
-        V.memset(tiny[:], TINY)
-        make_identity(nc, ident[:])
-        make_identity(nc, identb[:])
-        A.dma_start(out=ssb[:], in_=step_sizes.partition_broadcast(P))
-        A.dma_start(out=b2r[0:2, :], in_=b.partition_broadcast(2))
-        for jj in range(4):
-            for q in range(4):
+            cols = slice(2048 * i, 2048 * (i + 1))
+            nc.sync.dma_start(out=v_sb[:, cols], in_=v_init[:, cols])
+        nc.vector.memset(w_planes[:].rearrange("p j n -> p (j n)").bitcast(I32), 0)
+        nc.vector.memset(b_rows[:].bitcast(I32), 0)
+        nc.vector.memset(first_row[:], 0.0)
+        nc.vector.memset(first_row[0:1, :], 1.0)
+        nc.vector.memset(rho_cols[:], 0.0)
+        nc.vector.memset(minus_half[:], -0.5)
+        nc.vector.memset(tiny[:], TINY)
+        make_identity(nc, ident_f32[:])
+        make_identity(nc, ident_bf16[:])
+        nc.scalar.dma_start(out=step_logit[:], in_=step_sizes.partition_broadcast(P))
+        nc.scalar.dma_start(out=b_rows[0:2, :], in_=b.partition_broadcast(2))
+        for j in range(PASSES // 4):
+            for quarter in range(4):
                 nc.sync.dma_start(
-                    out=planes[32 * q:32 * q + 16, jj, :].bitcast(I32),
-                    in_=W_scales[4 * jj:4 * jj + 4, 4 * q:4 * q + 4, :].bitcast(I32),
+                    out=w_planes[32 * quarter:32 * quarter + 16, j, :].bitcast(I32),
+                    in_=W_scales[4 * j:4 * j + 4, 4 * quarter:4 * quarter + 4, :].bitcast(I32),
                 )
-        nc.sync.dma_start(out=z0[:], in_=z_0)
+        nc.sync.dma_start(out=z_sb[:], in_=z_0)
 
-        wtiles = []
+        w_tiles = []
 
-        def load_w(n):
-            wt = wpool.tile([P, NA], U32, name="wt%d" % n, tag="wt", align_bytes=64)
-            wtiles.append(wt)
-            dst = wt[:].bitcast(I32)
-            if n < G:
-                src = W_words[n].rearrange("p n t -> p (n t)")[:, 0:4 * NA].bitcast(I32)
+        def load_weights(n):
+            w_tile = weights.tile([P, N_FIRST], U32, name="w_tile%d" % n, tag="w_tile", align_bytes=64)
+            w_tiles.append(w_tile)
+            dst = w_tile[:].bitcast(I32)
+            if n < PASSES:
+                src = W_words[n].rearrange("p n t -> p (n t)")[:, 0:4 * N_FIRST].bitcast(I32)
                 nc.sync.dma_start(out=dst, in_=src)
             else:
-                g0 = 4 * (n - G)
-                cuts = [(0, 4)] if n < G + 3 else [(0, 2), (2, 3), (3, 4)]
-                dst3 = dst.rearrange("p (g c) -> p g c", g=4)
+                g0 = 4 * (n - PASSES)
+                cuts = [(0, 4)] if n < W_TILES - 1 else [(0, 2), (2, 3), (3, 4)]
+                dst_by_pass = dst.rearrange("p (g c) -> p g c", g=4)
                 for lo, hi in cuts:
-                    src = W_words[g0 + lo:g0 + hi].rearrange("g p n t -> p g (n t)")[:, :, 4 * NA:4 * N].bitcast(I32)
-                    nc.sync.dma_start(out=dst3[:, lo:hi, :], in_=src)
+                    src = W_words[g0 + lo:g0 + hi].rearrange("g p n t -> p g (n t)")[:, :, 4 * N_FIRST:4 * N]
+                    nc.sync.dma_start(out=dst_by_pass[:, lo:hi, :], in_=src.bitcast(I32))
 
-        for n in range(NW):
-            load_w(n)
+        for n in range(W_BUFS):
+            load_weights(n)
 
-        vw = v_sb[:].bitcast(F32)
-        xts = []
+        v_as_words = v_sb[:].bitcast(F32)
+        transposed = []
         for h in range(8):
-            xt = psum.tile([P, 2, 2, P], F32, name="xt%d" % h, tag="bank%d" % h)
-            xts.append(xt)
-            for gg in range(2):
-                g = 2 * h + gg
+            bank = psum.tile([P, 2, 2, P], F32, name="transposed%d" % h, tag="bank%d" % h)
+            transposed.append(bank)
+            for i in range(2):
+                g = 2 * h + i
                 for u in range(2):
-                    nc.tensor.transpose(xt[:, gg, u, :], vw[:, 256 * g + u:256 * (g + 1):2], ident[:])
+                    nc.tensor.transpose(bank[:, i, u, :], v_as_words[:, 256 * g + u:256 * (g + 1):2], ident_f32[:])
 
-        def copy_out(h):
-            dst = grouped[:, 2 * h:2 * h + 2, :, :]
-            src = xts[h][:].rearrange("p g u r -> p g r u")
+        def regroup(h):
+            dst = v_words[:, 2 * h:2 * h + 2, :, :]
+            src = transposed[h][:].rearrange("p g u r -> p g r u")
             if h % 2 == 0:
-                V.tensor_copy(out=dst, in_=src)
+                nc.vector.tensor_copy(out=dst, in_=src)
             else:
-                A.copy(out=dst, in_=src)
+                nc.scalar.copy(out=dst, in_=src)
 
-        def quant(i):
-            V.quantize_mx(
-                out=vcodes[:, 4 * i:4 * i + 4, :].rearrange("p g r -> p (g r)").bitcast(FP8X4),
-                scales=vscl[:, 4 * i:4 * i + 4, :].rearrange("p g r -> p (g r)"),
-                in_=grouped[:, 4 * i:4 * i + 4, :, :].rearrange("p g r u -> p (g r u)").bitcast(BF16),
+        def quantise(i):
+            four = slice(4 * i, 4 * i + 4)
+            nc.vector.quantize_mx(
+                out=v_codes[:, four, :].rearrange("p g r -> p (g r)").bitcast(FP8X4),
+                scales=v_scales[:, four, :].rearrange("p g r -> p (g r)"),
+                in_=v_words[:, four, :, :].rearrange("p g r u -> p (g r u)").bitcast(BF16),
             )
 
-        copy_out(0)
-        copy_out(1)
-        copy_out(2)
-        copy_out(3)
-        quant(0)
-        copy_out(4)
-        copy_out(5)
-        quant(1)
-        copy_out(6)
-        copy_out(7)
-        quant(2)
-        quant(3)
+        regroup(0)
+        regroup(1)
+        for i in range(3):
+            regroup(2 * i + 2)
+            regroup(2 * i + 3)
+            quantise(i)
+        quantise(3)
 
-        for c in range(5):
-            pb = psum.tile([P, CH], F32, name="pb%d" % c, tag="bank%d" % (4 + c % 4))
-            nc.tensor.matmul(pb[:], lhsT=sel[:], rhs=b2r[:, CH * c:CH * (c + 1)], start=True, stop=True)
-            A.copy(out=bbc[:, CH * c:CH * (c + 1)], in_=pb[:])
+        for c in range(CHUNKS):
+            bank = psum.tile([P, BANK], F32, name="b_bank%d" % c, tag="bank%d" % (4 + c % 4))
+            nc.tensor.matmul(bank[:], lhsT=first_row[:], rhs=b_rows[:, chunk(c)], start=True, stop=True)
+            nc.scalar.copy(out=b_all[:, chunk(c)], in_=bank[:])
 
-        v2c = sm("v2c", 4)
+        vv_parts = row_value("vv_parts", 4)
         for i in range(4):
-            A.activation(out=junk_a[:, 0:2048], in_=v_sb[:, 2048 * i:2048 * (i + 1)], func=ACTF.Square,
-                         accum_out=v2c[:, i:i + 1])
-        b2 = sm("b2")
-        A.activation(out=junk_a[:], in_=bbc[:], func=ACTF.Square, accum_out=b2[:])
-        z2 = sm("z2")
-        A.activation(out=junk_a[:], in_=z0[:], func=ACTF.Square, accum_out=z2[:])
-        zbc = sm("zbc", 5)
-        for c in range(5):
-            stt(junk_v[:], z0[:, CH * c:CH * (c + 1)], 1.0, bbc[:, CH * c:CH * (c + 1)], ALU.mult, ALU.mult,
-                acc=zbc[:, c:c + 1])
-        zb = sm("zb")
-        V.tensor_reduce(out=zb[:], in_=zbc[:], axis=AX.X, op=ALU.add)
+            nc.scalar.activation(out=scrap_s[:, 0:2048], in_=v_sb[:, 2048 * i:2048 * (i + 1)], func=ACT.Square,
+                                 accum_out=vv_parts[:, i:i + 1])
+        bb = row_value("bb")
+        nc.scalar.activation(out=scrap_s[:], in_=b_all[:], func=ACT.Square, accum_out=bb[:])
+        zz = row_value("zz")
+        nc.scalar.activation(out=scrap_s[:], in_=z_sb[:], func=ACT.Square, accum_out=zz[:])
+        zb_parts = row_value("zb_parts", CHUNKS)
+        for c in range(CHUNKS):
+            fused(scrap_v[:], z_sb[:, chunk(c)], ALU.mult, 1.0, ALU.mult, b_all[:, chunk(c)], total=zb_parts[:, c:c + 1])
+        zb = row_value("zb")
+        nc.vector.tensor_reduce(out=zb[:], in_=zb_parts[:], axis=AX.X, op=ALU.add)
 
-        v2 = sm("v2")
-        V.tensor_reduce(out=v2[:], in_=v2c[:], axis=AX.X, op=ALU.add)
-        v2m = sm("v2m")
-        ts(v2m[:], v2[:], EPS2, None, ALU.max)
-        rvn = sm("rvn")
-        nc.gpsimd.tensor_tensor(out=rvn[:], in0=v2m[:], in1=mh[:, 0:1], op=ALU.pow)
-        cl = sm("cl")
-        ts(cl[:], v2m[:], rvn[:], MAXN, ALU.mult, ALU.min)
-        onem = sm("onem")
-        ts(onem[:], cl[:], -1.0, 1.0, ALU.mult, ALU.add)
-        rom = sm("rom")
-        V.reciprocal(out=rom[:], in_=onem[:])
-        ratio = sm("ratio")
-        stt(ratio[:], cl[:], 1.0, rom[:], ALU.add, ALU.mult)
-        lnr = sm("lnr")
-        A.activation(out=lnr[:], in_=ratio[:], func=ACTF.Ln)
-        r = sm("r")
-        stt(r[:], lnr[:], 0.5, rvn[:], ALU.mult, ALU.mult)
+        vv = row_value("vv")
+        nc.vector.tensor_reduce(out=vv[:], in_=vv_parts[:], axis=AX.X, op=ALU.add)
+        vv_c = row_value("vv_c")
+        scal(vv_c[:], vv[:], EPS_SQ, ALU.max)
+        inv_vn = row_value("inv_vn")
+        inverse_root(inv_vn[:], vv_c[:])
+        vn_c = row_value("vn_c")
+        scal(vn_c[:], vv_c[:], inv_vn[:], ALU.mult, MAX_NORM, ALU.min)
+        one_minus = row_value("one_minus")
+        scal(one_minus[:], vn_c[:], -1.0, ALU.mult, 1.0, ALU.add)
+        inv_one_minus = row_value("inv_one_minus")
+        inverse(inv_one_minus[:], one_minus[:])
+        ratio = row_value("ratio")
+        fused(ratio[:], vn_c[:], ALU.add, 1.0, ALU.mult, inv_one_minus[:])
+        log_ratio = row_value("log_ratio")
+        nc.scalar.activation(out=log_ratio[:], in_=ratio[:], func=ACT.Ln)
+        gain = row_value("gain")
+        fused(gain[:], log_ratio[:], ALU.mult, 0.5, ALU.mult, inv_vn[:])
 
-        b2m = sm("b2m")
-        ts(b2m[:], b2[:], EPS2, None, ALU.max)
-        rbn = sm("rbn")
-        nc.gpsimd.tensor_tensor(out=rbn[:], in0=b2m[:], in1=mh[:, 0:1], op=ALU.pow)
-        bn = sm("bn")
-        tt(bn[:], b2m[:], rbn[:], ALU.mult)
-        ths = sm("ths")
-        A.activation(out=ths[:], in_=ssb[:], func=ACTF.Tanh, scale=0.5)
-        tb = sm("tb")
-        A.activation(out=tb[:], in_=bn[:], func=ACTF.Tanh)
-        beta = sm("beta")
-        tt(beta[:], tb[:], rbn[:], ALU.mult)
-        beta2 = sm("beta2")
-        ts(beta2[:], beta[:], 2.0, None, ALU.mult)
-        y2 = sm("y2")
-        stt(y2[:], beta[:], beta[:], b2[:], ALU.mult, ALU.mult)
-        stept = sm("stept", 2)
-        ts(stept[:, 0:1], ths[:], 0.5, 0.5, ALU.mult, ALU.add)
-        ts(stept[:, 1:2], ths[:], 1.0, None, ALU.add)
-        qz = sm("qz")
-        ts(qz[:], z2[:], -1.0, 1.0, ALU.mult, ALU.add)
-        qzm = sm("qzm")
-        ts(qzm[:], qz[:], EPS, None, ALU.max)
-        hl = sm("hl")
-        V.reciprocal(out=hl[:], in_=qzm[:])
-        se = sm("se", 2)
-        ts(se[:], stept[:], 1.0 / EPS, None, ALU.mult)
-        xq1 = small.tile([P, 3, 3], F32, name="xq1")
-        cq1 = small.tile([P, 3, 3], F32, name="cq1")
-        oq1 = small.tile([P, 3, 3], F32, name="oq1")
-        xq2 = small.tile([P, 2, 3, 3], F32, name="xq2")
-        cq2 = small.tile([P, 2, 3, 3], F32, name="cq2")
-        oq2 = small.tile([P, 2, 3, 3], F32, name="oq2")
-        V.memset(xq1[:], 0.0)
-        V.memset(xq2[:], 0.0)
-        V.memset(cq1[:], 0.0)
-        V.memset(cq1[:, 0, 0:1], 1.0)
-        V.memset(cq1[:, 1, 2:3], 1.0)
-        ts(cq1[:, 1, 0:1], y2[:], 0.0, None, ALU.add)
-        ts(cq1[:, 0, 2:3], y2[:], 0.0, None, ALU.add)
-        ts(cq1[:, 2, 2:3], y2[:], 1.0, None, ALU.add)
-        V.memset(cq2[:], 1.0)
-        ts(cq2[:, :, 1, 2], z2[:].to_broadcast([P, 2]), 0.0, None, ALU.add)
+        bb_c = row_value("bb_c")
+        scal(bb_c[:], bb[:], EPS_SQ, ALU.max)
+        inv_bn = row_value("inv_bn")
+        inverse_root(inv_bn[:], bb_c[:])
+        bn = row_value("bn")
+        pair(bn[:], bb_c[:], ALU.mult, inv_bn[:])
+        tanh_half = row_value("tanh_half")
+        nc.scalar.activation(out=tanh_half[:], in_=step_logit[:], func=ACT.Tanh, scale=0.5)
+        tanh_bn = row_value("tanh_bn")
+        nc.scalar.activation(out=tanh_bn[:], in_=bn[:], func=ACT.Tanh)
+        beta = row_value("beta")
+        pair(beta[:], tanh_bn[:], ALU.mult, inv_bn[:])
+        two_beta = row_value("two_beta")
+        scal(two_beta[:], beta[:], 2.0, ALU.mult)
+        y2 = row_value("y2")
+        fused(y2[:], beta[:], ALU.mult, beta[:], ALU.mult, bb[:])
+        steps = row_value("steps", 2)
+        scal(steps[:, 0:1], tanh_half[:], 0.5, ALU.mult, 0.5, ALU.add)
+        scal(steps[:, 1:2], tanh_half[:], 1.0, ALU.add)
+        one_minus_zz = row_value("one_minus_zz")
+        scal(one_minus_zz[:], zz[:], -1.0, ALU.mult, 1.0, ALU.add)
+        one_minus_zz_c = row_value("one_minus_zz_c")
+        scal(one_minus_zz_c[:], one_minus_zz[:], EPS, ALU.max)
+        half_lam = row_value("half_lam")
+        inverse(half_lam[:], one_minus_zz_c[:])
+        steps_over_eps = row_value("steps_over_eps", 2)
+        scal(steps_over_eps[:], steps[:], 1.0 / EPS, ALU.mult)
+
+        x_first = rows.tile([P, 3, 3], F32, name="x_first")
+        abc_first = rows.tile([P, 3, 3], F32, name="abc_first")
+        val_first = rows.tile([P, 3, 3], F32, name="val_first")
+        x_second = rows.tile([P, 2, 3, 3], F32, name="x_second")
+        abc_second = rows.tile([P, 2, 3, 3], F32, name="abc_second")
+        val_second = rows.tile([P, 2, 3, 3], F32, name="val_second")
+        nc.vector.memset(x_first[:], 0.0)
+        nc.vector.memset(x_second[:], 0.0)
+        nc.vector.memset(abc_first[:], 0.0)
+        nc.vector.memset(abc_first[:, 0, 0:1], 1.0)
+        nc.vector.memset(abc_first[:, 1, 2:3], 1.0)
+        scal(abc_first[:, 1, 0:1], y2[:], 0.0, ALU.add)
+        scal(abc_first[:, 0, 2:3], y2[:], 0.0, ALU.add)
+        scal(abc_first[:, 2, 2:3], y2[:], 1.0, ALU.add)
+        nc.vector.memset(abc_second[:], 1.0)
+        scal(abc_second[:, :, 1, 2], zz[:].to_broadcast([P, 2]), 0.0, ALU.add)
 
         acc = []
-        for j in range(5):
-            at = psum.tile([P, CH], F32, name="acc%d" % j, tag="bank%d" % j)
-            acc.append(at)
+        for c in range(CHUNKS):
+            bank = psum.tile([P, BANK], F32, name="acc%d" % c, tag="bank%d" % c)
+            acc.append(bank)
 
-        def mx(g, j, wt, col):
-            k = 4 * (g % 4)
+        def mx_pass(g, c, w_tile, col):
             nc.tensor.matmul_mx(
-                out=acc[j][:],
-                lhsT=vcodes[:, g, :].bitcast(FP8X4),
-                lhsT_scale=vscl[:, g, :],
-                rhs=wt[:, col:col + CH].bitcast(FP8X4),
-                rhs_scale=planes[k:P, g // 4, CH * j:CH * (j + 1)],
+                out=acc[c][:],
+                lhsT=v_codes[:, g, :].bitcast(FP8X4),
+                lhsT_scale=v_scales[:, g, :],
+                rhs=w_tile[:, col:col + BANK].bitcast(FP8X4),
+                rhs_scale=w_planes[4 * (g % 4):P, g // 4, chunk(c)],
                 start=(g == 0),
-                stop=(g == G - 1),
+                stop=(g == PASSES - 1),
             )
 
-        wps = []
+        s_parts = row_value("s_parts", LAST)
+        d_parts = row_value("d_parts", LAST)
+        z_parts = row_value("z_parts", LAST)
+        s_first = row_value("s_first")
+        d_first = row_value("d_first")
+        z_first = row_value("z_first")
 
-        def w_open(c):
-            wp = psum.tile([P, CH], F32, name="wp%d" % c, tag="bank%d" % c)
-            wps.append(wp)
-            cs = slice(CH * c, CH * (c + 1))
-            nc.tensor.matmul(wp[:], lhsT=ident[:], rhs=mv[:, cs], start=True, stop=False)
+        def sums_over_first_block():
+            for c in range(LAST):
+                nc.scalar.copy(out=mv_first[:, chunk(c)], in_=acc[c][:])
+                nc.scalar.activation(out=scrap_s[:, 0:BANK], in_=acc[c][:], func=ACT.Square,
+                                     accum_out=s_parts[:, c:c + 1])
+                fused(scrap_v[:], mv_first[:, chunk(c)], ALU.mult, 1.0, ALU.mult, b_all[:, chunk(c)],
+                      total=d_parts[:, c:c + 1])
+                fused(scrap_v[:], mv_first[:, chunk(c)], ALU.mult, 1.0, ALU.mult, z_sb[:, chunk(c)],
+                      total=z_parts[:, c:c + 1])
+            nc.vector.tensor_reduce(out=s_first[:], in_=s_parts[:], axis=AX.X, op=ALU.add)
+            nc.vector.tensor_reduce(out=d_first[:], in_=d_parts[:], axis=AX.X, op=ALU.add)
+            nc.vector.tensor_reduce(out=z_first[:], in_=z_parts[:], axis=AX.X, op=ALU.add)
 
-        def w_close(c):
-            nc.tensor.matmul(wps[c][:], lhsT=lt[:], rhs=b2r[:, CH * c:CH * (c + 1)], start=False, stop=True)
-
-        for n in range(G + 4):
-            if n < G:
-                for j in range(4):
-                    mx(n, j, wtiles[n], CH * j)
+        for n in range(W_TILES):
+            if n < PASSES:
+                for c in range(LAST):
+                    mx_pass(n, c, w_tiles[n], BANK * c)
             else:
                 for i in range(4):
-                    mx(4 * (n - G) + i, 4, wtiles[n], CH * i)
-            if n + NW < G + 4:
-                load_w(n + NW)
-            if n == G - 1:
-                sac = sm("sac", 4)
-                dac = sm("dac", 4)
-                zac = sm("zac", 4)
-                for j in range(4):
-                    cs = slice(CH * j, CH * (j + 1))
-                    A.copy(out=mv[:, cs], in_=acc[j][:])
-                    A.activation(out=junk_a[:, 0:CH], in_=acc[j][:], func=ACTF.Square, accum_out=sac[:, j:j + 1])
-                    stt(junk_v[:], mv[:, cs], 1.0, bbc[:, cs], ALU.mult, ALU.mult, acc=dac[:, j:j + 1])
-                    stt(junk_v[:], mv[:, cs], 1.0, z0[:, cs], ALU.mult, ALU.mult, acc=zac[:, j:j + 1])
-                sa = sm("sa")
-                V.tensor_reduce(out=sa[:], in_=sac[:], axis=AX.X, op=ALU.add)
-                sap = sm("sap")
-                ts(sap[:], sa[:], EPS2, None, ALU.add)
-                da = sm("da")
-                V.tensor_reduce(out=da[:], in_=dac[:], axis=AX.X, op=ALU.add)
-                za = sm("za")
-                V.tensor_reduce(out=za[:], in_=zac[:], axis=AX.X, op=ALU.add)
-        for c in range(4):
-            w_open(c)
+                    mx_pass(4 * (n - PASSES) + i, LAST, w_tiles[n], BANK * i)
+            if n + W_BUFS < W_TILES:
+                load_weights(n + W_BUFS)
+            if n == PASSES - 1:
+                sums_over_first_block()
 
-        GP = nc.gpsimd
-        csb = slice(NA, N)
-        sb = sm("sb")
-        A.activation(out=junk_a[:, 0:CH], in_=acc[4][:], func=ACTF.Square, accum_out=sb[:])
-        sx = sm("sx")
-        tt(sx[:], sb[:], sap[:], ALU.add)
-        rm = sm("rm")
-        GP.tensor_tensor(out=rm[:], in0=sx[:], in1=mh[:, 0:1], op=ALU.pow)
-        rs_ = sm("rs_")
-        ts(rs_[:], sb[:], sap[:], r[:], ALU.add, ALU.mult)
-        A.activation(out=xq1[:, :, 1:3], in_=rm[:].unsqueeze(2).to_broadcast([P, 3, 2]), func=ACTF.Tanh, scale=rs_[:])
-        th = xq1[:, 0, 1:2]
-        db = sm("db")
-        stt(junk_v[:], acc[4][:], 1.0, bbc[:, csb], ALU.mult, ALU.mult, acc=db[:])
-        d2 = sm("d2")
-        ts(d2[:], db[:], da[:], beta2[:], ALU.add, ALU.mult)
-        ts(cq1[:, :, 1], d2[:].to_broadcast([P, 3]), rm[:], None, ALU.mult)
-        V.tensor_tensor_scan(
-            out=oq1[:].rearrange("p g e -> p (g e)"),
-            data0=xq1[:].rearrange("p g e -> p (g e)"),
-            data1=cq1[:].rearrange("p g e -> p (g e)"),
-            initial=0.0, op0=ALU.mult, op1=ALU.add,
-        )
-        n1 = oq1[:, 0, 2:3]
-        den0 = oq1[:, 1, 2:3]
-        pp = oq1[:, 2, 2:3]
-        ndm = sm("ndm")
-        stt(ndm[:], n1, den0, tiny[:], ALU.mult, ALU.max)
-        rs = sm("rs")
-        GP.tensor_tensor(out=rs[:], in0=ndm[:], in1=mh[:, 0:1], op=ALU.pow)
-        dmax = sm("dmax")
-        ts(dmax[:], den0, EPS, None, ALU.max)
-        al = sm("al")
-        tt(al[:], th, rm[:], ALU.mult)
-        qq = sm("qq")
-        tt(qq[:], pp, n1, ALU.subtract)
-        rden = sm("rden")
-        V.reciprocal(out=rden[:], in_=dmax[:])
-        e1 = sm("e1")
-        tt(e1[:], pp, al[:], ALU.mult)
-        e2 = sm("e2")
-        tt(e2[:], qq[:], beta[:], ALU.mult)
-        ndr = sm("ndr")
-        tt(ndr[:], ndm[:], rden[:], ALU.mult)
-        re1 = sm("re1")
-        V.reciprocal(out=re1[:], in_=e1[:])
-        zq = sm("zq")
-        tt(zq[:], e1[:], za[:], ALU.mult)
-        qe = sm("qe")
-        tt(qe[:], e1[:], qz[:], ALU.mult)
-        rho = sm("rho")
-        tt(rho[:], e2[:], re1[:], ALU.mult)
-        tt(lp[:, 0:1], e2[:], re1[:], ALU.mult)
-        zp = sm("zp")
-        stt(zp[:], e2[:], zb[:], zq[:], ALU.mult, ALU.add)
-        tt(lp[:, 1:2], rho[:], lp[:, 0:1], ALU.subtract)
-        zbb = sm("zbb")
-        stt(junk_v[:], acc[4][:], 1.0, z0[:, csb], ALU.mult, ALU.mult, acc=zbb[:])
-        ltp = psum.tile([P, P], BF16, name="ltp", tag="bank5")
-        nc.tensor.transpose(ltp[:], lp[:], identb[:])
-        v0n = sm("v0n")
-        ts(v0n[:], rs[:], ndr[:], MAXN, ALU.mult, ALU.min)
-        rv0 = sm("rv0")
-        ts(rv0[:], rs[:], dmax[:], 1.0 / MAXN, ALU.mult, ALU.max)
-        sc = sm("sc")
-        stt(sc[:], rs[:], MAXN, rden[:], ALU.mult, ALU.min)
-        zz2 = sm("zz2")
-        stt(zz2[:], zbb[:], e1[:], zp[:], ALU.mult, ALU.add)
-        vtn = sm("vtn", 2)
-        ts(vtn[:], stept[:], v0n[:], EPS, ALU.mult, ALU.max)
-        A.activation(out=xq2[:, :, :, 1:3], in_=vtn[:].unsqueeze(2).unsqueeze(3).to_broadcast([P, 2, 3, 2]),
-                     func=ACTF.Tanh, scale=hl[:])
-        tht = xq2[:, :, 0, 1]
-        s2 = sm("s2", 2)
-        ts(s2[:], se[:], v0n[:], 1.0, ALU.mult, ALU.min)
-        qt = sm("qt", 2)
-        ts(qt[:], se[:], rv0[:], None, ALU.min)
-        zv2 = sm("zv2")
-        stt(zv2[:], zz2[:], 2.0, sc[:], ALU.mult, ALU.mult)
-        sqe1 = sm("sqe1")
-        tt(sqe1[:], sc[:], qe[:], ALU.mult)
-        s2b = s2[:].unsqueeze(2).to_broadcast([P, 2, 2])
-        tt(cq2[:, :, 0:2, 0], s2b, s2b, ALU.mult)
-        stt(cq2[:, :, 2, 0], s2[:], z2[:], s2[:], ALU.mult, ALU.mult)
-        ts(cq2[:, :, :, 1], qt[:].unsqueeze(2).to_broadcast([P, 2, 3]), zv2[:], None, ALU.mult)
-        q1 = sm("q1", 2)
-        ts(q1[:], qt[:], sqe1[:], TINY, ALU.mult, ALU.add)
-        rq1 = sm("rq1", 2)
-        V.reciprocal(out=rq1[:], in_=q1[:])
-        V.tensor_copy(out=lt[:], in_=ltp[:])
-        for c in range(4):
-            w_close(c)
-        V.tensor_tensor_scan(
-            out=oq2[:].rearrange("p t g e -> p (t g e)"),
-            data0=xq2[:].rearrange("p t g e -> p (t g e)"),
-            data1=cq2[:].rearrange("p t g e -> p (t g e)"),
-            initial=0.0, op0=ALU.mult, op1=ALU.add,
-        )
-        rt = sm("rt", 2)
-        V.reciprocal(out=rt[:], in_=tht)
-        jt = sm("jt", 2)
-        ndtm = sm("ndtm", 2)
-        for t in range(2):
-            stt(jt[:, t:t + 1], oq2[:, t, 0, 2:3], rt[:, t:t + 1], rq1[:, t:t + 1], ALU.mult, ALU.mult)
-        for t in range(2):
-            stt(ndtm[:, t:t + 1], oq2[:, t, 1, 2:3], oq2[:, t, 2, 2:3], tiny[:], ALU.mult, ALU.max)
-        rst = sm("rst", 2)
-        GP.tensor_tensor(out=rst[:], in0=ndtm[:], in1=mh[:], op=ALU.pow)
-        dmt = sm("dmt", 2)
-        ts(dmt[:], oq2[:, :, 2, 2], EPS, None, ALU.max)
-        g1 = sm("g1", 2)
-        tt(g1[:], tht, q1[:], ALU.mult)
-        rdt = sm("rdt", 2)
-        V.reciprocal(out=rdt[:], in_=dmt[:])
-        sct = sm("sct", 2)
-        ca = sm("ca", 2)
+        w_banks = []
+        for c in range(LAST):
+            bank = psum.tile([P, BANK], F32, name="w_bank%d" % c, tag="bank%d" % c)
+            w_banks.append(bank)
+            nc.tensor.matmul(bank[:], lhsT=ident_f32[:], rhs=mv_first[:, chunk(c)], start=True, stop=False)
 
-        order = [(c, t) for c in range(5) for t in range(2)]
-        for i in range(10):
-            c, t = order[i]
-            cs = slice(CH * c, CH * (c + 1))
-            if i == 8:
-                stt(wb[:], bbc[:, csb], rho[:], acc[4][:], ALU.mult, ALU.add)
-            ut = tpool.tile([P, CH], F32, name="ut%d_%d" % (c, t), tag="ut")
-            src = wps[c][:] if c < 4 else wb[:]
-            stt(ut[:], z0[:, cs], jt[:, t:t + 1], src, ALU.mult, ALU.add)
-            if i == 0:
-                stt(sct[:], rst[:], MAXN, rdt[:], ALU.mult, ALU.min)
-                tt(ca[:], sct[:], g1[:], ALU.mult)
-            ot = opool.tile([P, CH], F32, name="ot%d_%d" % (c, t), tag="ot")
-            A.activation(out=ot[:], in_=ut[:], func=ACTF.Copy, scale=ca[:, t:t + 1])
-            nc.sync.dma_start(out=out[:, t, cs], in_=ot[:])
+        s_last = row_value("s_last")
+        nc.scalar.activation(out=scrap_s[:, 0:BANK], in_=acc[LAST][:], func=ACT.Square, accum_out=s_last[:])
+        s_c = row_value("s_c")
+        scal(s_c[:], s_last[:], s_first[:], ALU.add, EPS_SQ, ALU.max)
+        inv_m = row_value("inv_m")
+        inverse_root(inv_m[:], s_c[:])
+        gain_s = row_value("gain_s")
+        pair(gain_s[:], s_c[:], ALU.mult, gain[:])
+        nc.scalar.activation(out=x_first[:, :, 1:3], in_=inv_m[:].unsqueeze(2).to_broadcast([P, 3, 2]), func=ACT.Tanh,
+                             scale=gain_s[:])
+        th = x_first[:, 0, 1:2]
+        d_last = row_value("d_last")
+        fused(scrap_v[:], acc[LAST][:], ALU.mult, 1.0, ALU.mult, b_all[:, chunk(LAST)], total=d_last[:])
+        d_beta = row_value("d_beta")
+        scal(d_beta[:], d_last[:], d_first[:], ALU.add, two_beta[:], ALU.mult)
+        scal(abc_first[:, :, 1], d_beta[:].to_broadcast([P, 3]), inv_m[:], ALU.mult)
+
+        horner(val_first[:].rearrange("p f e -> p (f e)"), x_first[:].rearrange("p f e -> p (f e)"),
+               abc_first[:].rearrange("p f e -> p (f e)"))
+        norm1 = val_first[:, 0, 2:3]
+        den1 = val_first[:, 1, 2:3]
+        coef_x = val_first[:, 2, 2:3]
+        nd1 = row_value("nd1")
+        fused(nd1[:], norm1, ALU.mult, den1, ALU.max, tiny[:])
+        inv_root1 = row_value("inv_root1")
+        inverse_root(inv_root1[:], nd1[:])
+        den1_c = row_value("den1_c")
+        scal(den1_c[:], den1, EPS, ALU.max)
+        alpha = row_value("alpha")
+        pair(alpha[:], th, ALU.mult, inv_m[:])
+        one_minus_x2 = row_value("one_minus_x2")
+        pair(one_minus_x2[:], coef_x, ALU.subtract, norm1)
+        inv_den1 = row_value("inv_den1")
+        inverse(inv_den1[:], den1_c[:])
+        e1 = row_value("e1")
+        pair(e1[:], coef_x, ALU.mult, alpha[:])
+        e2 = row_value("e2")
+        pair(e2[:], one_minus_x2[:], ALU.mult, beta[:])
+        nd1_over_den = row_value("nd1_over_den")
+        pair(nd1_over_den[:], nd1[:], ALU.mult, inv_den1[:])
+        inv_e1 = row_value("inv_e1")
+        inverse(inv_e1[:], e1[:])
+        e1_z_first = row_value("e1_z_first")
+        pair(e1_z_first[:], e1[:], ALU.mult, z_first[:])
+        e1_q = row_value("e1_q")
+        pair(e1_q[:], e1[:], ALU.mult, one_minus_zz[:])
+        rho = row_value("rho")
+        pair(rho[:], e2[:], ALU.mult, inv_e1[:])
+        pair(rho_cols[:, 0:1], e2[:], ALU.mult, inv_e1[:])
+        z_num_first = row_value("z_num_first")
+        fused(z_num_first[:], e2[:], ALU.mult, zb[:], ALU.add, e1_z_first[:])
+        pair(rho_cols[:, 1:2], rho[:], ALU.subtract, rho_cols[:, 0:1])
+        z_last = row_value("z_last")
+        fused(scrap_v[:], acc[LAST][:], ALU.mult, 1.0, ALU.mult, z_sb[:, chunk(LAST)], total=z_last[:])
+        rho_bank = psum.tile([P, P], BF16, name="rho_bank", tag="bank5")
+        nc.tensor.transpose(rho_bank[:], rho_cols[:], ident_bf16[:])
+
+        v0_norm = row_value("v0_norm")
+        scal(v0_norm[:], inv_root1[:], nd1_over_den[:], ALU.mult, MAX_NORM, ALU.min)
+        inv_v0 = row_value("inv_v0")
+        scal(inv_v0[:], inv_root1[:], den1_c[:], ALU.mult, 1.0 / MAX_NORM, ALU.max)
+        scale1 = row_value("scale1")
+        fused(scale1[:], inv_root1[:], ALU.mult, MAX_NORM, ALU.min, inv_den1[:])
+        z_num = row_value("z_num")
+        fused(z_num[:], z_last[:], ALU.mult, e1[:], ALU.add, z_num_first[:])
+        vt_norm = row_value("vt_norm", 2)
+        scal(vt_norm[:], steps[:], v0_norm[:], ALU.mult, EPS, ALU.max)
+        nc.scalar.activation(out=x_second[:, :, :, 1:3],
+                             in_=vt_norm[:].unsqueeze(2).unsqueeze(3).to_broadcast([P, 2, 3, 2]),
+                             func=ACT.Tanh, scale=half_lam[:])
+        tht = x_second[:, :, 0, 1]
+
+        gamma_v0 = row_value("gamma_v0", 2)
+        scal(gamma_v0[:], steps_over_eps[:], v0_norm[:], ALU.mult, 1.0, ALU.min)
+        gamma = row_value("gamma", 2)
+        scal(gamma[:], steps_over_eps[:], inv_v0[:], ALU.min)
+        two_z_v0 = row_value("two_z_v0")
+        fused(two_z_v0[:], z_num[:], ALU.mult, 2.0, ALU.mult, scale1[:])
+        scale1_e1_q = row_value("scale1_e1_q")
+        pair(scale1_e1_q[:], scale1[:], ALU.mult, e1_q[:])
+        twice = gamma_v0[:].unsqueeze(2).to_broadcast([P, 2, 2])
+        pair(abc_second[:, :, 0:2, 0], twice, ALU.mult, twice)
+        fused(abc_second[:, :, 2, 0], gamma_v0[:], ALU.mult, zz[:], ALU.mult, gamma_v0[:])
+        scal(abc_second[:, :, :, 1], gamma[:].unsqueeze(2).to_broadcast([P, 2, 3]), two_z_v0[:], ALU.mult)
+        g_over_tht = row_value("g_over_tht", 2)
+        scal(g_over_tht[:], gamma[:], scale1_e1_q[:], ALU.mult, TINY, ALU.add)
+        inv_g_over_tht = row_value("inv_g_over_tht", 2)
+        inverse(inv_g_over_tht[:], g_over_tht[:])
+        nc.vector.tensor_copy(out=rho_rows[:], in_=rho_bank[:])
+        for c in range(LAST):
+            nc.tensor.matmul(w_banks[c][:], lhsT=rho_rows[:], rhs=b_rows[:, chunk(c)], start=False, stop=True)
+
+        horner(val_second[:].rearrange("p t f e -> p (t f e)"), x_second[:].rearrange("p t f e -> p (t f e)"),
+               abc_second[:].rearrange("p t f e -> p (t f e)"))
+        inv_tht = row_value("inv_tht", 2)
+        inverse(inv_tht[:], tht)
+        j_t = row_value("j_t", 2)
+        nd2 = row_value("nd2", 2)
+        for t in range(2):
+            fused(j_t[:, t:t + 1], val_second[:, t, 0, 2:3], ALU.mult, inv_tht[:, t:t + 1], ALU.mult,
+                  inv_g_over_tht[:, t:t + 1])
+        for t in range(2):
+            fused(nd2[:, t:t + 1], val_second[:, t, 1, 2:3], ALU.mult, val_second[:, t, 2, 2:3], ALU.max, tiny[:])
+        inv_root2 = row_value("inv_root2", 2)
+        inverse_root(inv_root2[:], nd2[:], cols=2)
+        den2_c = row_value("den2_c", 2)
+        scal(den2_c[:], val_second[:, :, 2, 2], EPS, ALU.max)
+        g_t = row_value("g_t", 2)
+        pair(g_t[:], tht, ALU.mult, g_over_tht[:])
+        inv_den2 = row_value("inv_den2", 2)
+        inverse(inv_den2[:], den2_c[:])
+        scale2 = row_value("scale2", 2)
+        a_t = row_value("a_t", 2)
+
+        for c in range(CHUNKS):
+            if c == LAST:
+                fused(w_last[:], b_all[:, chunk(LAST)], ALU.mult, rho[:], ALU.add, acc[LAST][:])
+            for t in range(2):
+                sum_t = unscaled.tile([P, BANK], F32, name="sum%d_%d" % (c, t), tag="sum")
+                w = w_banks[c][:] if c < LAST else w_last[:]
+                fused(sum_t[:], z_sb[:, chunk(c)], ALU.mult, j_t[:, t:t + 1], ALU.add, w)
+                if c == 0 and t == 0:
+                    fused(scale2[:], inv_root2[:], ALU.mult, MAX_NORM, ALU.min, inv_den2[:])
+                    pair(a_t[:], scale2[:], ALU.mult, g_t[:])
+                out_t = scaled.tile([P, BANK], F32, name="out%d_%d" % (c, t), tag="out")
+                nc.scalar.activation(out=out_t[:], in_=sum_t[:], func=ACT.Copy, scale=a_t[:, t:t + 1])
+                nc.sync.dma_start(out=out[:, t, chunk(c)], in_=out_t[:])

from contextlib import ExitStack

import concourse.mybir as mybir
from concourse.masks import make_identity

F32 = mybir.dt.float32
BF16 = mybir.dt.bfloat16
I32 = mybir.dt.int32
U32 = mybir.dt.uint32
U8 = mybir.dt.uint8
FP8X4 = mybir.dt.float8_e4m3fn_x4
ALU = mybir.AluOpType
ACT = mybir.ActivationFunctionType
AX = mybir.AxisListType

P = 128
K = 8192
N = 2560
PASSES = K // 512
BANK = 512
N_FIRST = 2048
CHUNKS = N // BANK
LAST = CHUNKS - 1
W_TILES = PASSES + PASSES // 4
W_BUFS = 12
EPS = 1e-7
EPS_SQ = 1e-14
MAX_NORM = 1.0 - 1e-5
TINY = 1e-30

FLOPS = 2 * P * K * N


def tile_paralleldirectpoincaredynamics_w_kernel(tc, z_0, v_init, W_words, W_scales, b, step_sizes, out):
    nc = tc.nc
    with ExitStack() as ctx:
        ctx.enter_context(tc.manual_schedule())
        keep = ctx.enter_context(tc.tile_pool(name="keep", bufs=1))
        rows = ctx.enter_context(tc.tile_pool(name="rows", bufs=1))
        weights = ctx.enter_context(tc.tile_pool(name="weights", bufs=W_BUFS))
        unscaled = ctx.enter_context(tc.tile_pool(name="unscaled", bufs=4))
        scaled = ctx.enter_context(tc.tile_pool(name="scaled", bufs=2 * CHUNKS))
        psum = ctx.enter_context(tc.psum_pool(name="psum", bufs=1))

        def row_value(name, cols=1):
            return rows.tile([P, cols], F32, name=name)

        def scal(o, i, s1, op0, s2=None, op1=None):
            if op1 is None:
                nc.vector.tensor_scalar(out=o, in0=i, scalar1=s1, scalar2=None, op0=op0)
            else:
                nc.vector.tensor_scalar(out=o, in0=i, scalar1=s1, scalar2=s2, op0=op0, op1=op1)

        def fused(o, i0, op0, s, op1, i1, total=None):
            nc.vector.scalar_tensor_tensor(out=o, in0=i0, scalar=s, in1=i1, op0=op0, op1=op1, accum_out=total)

        def pair(o, i0, op, i1):
            nc.vector.tensor_tensor(out=o, in0=i0, in1=i1, op=op)

        def inverse(o, i):
            nc.vector.reciprocal(out=o, in_=i)

        def inverse_root(o, i, cols=1):
            nc.gpsimd.tensor_tensor(out=o, in0=i, in1=minus_half[:, 0:cols], op=ALU.pow)

        def horner(o, x, abc):
            nc.vector.tensor_tensor_scan(out=o, data0=x, data1=abc, initial=0.0, op0=ALU.mult, op1=ALU.add)

        def chunk(c):
            return slice(BANK * c, BANK * (c + 1))

        v_sb = keep.tile([P, K], BF16, name="v_sb", align_bytes=64)
        v_words = keep.tile([P, PASSES, P, 2], F32, name="v_words", align_bytes=64)
        v_codes = keep.tile([P, PASSES, P], U32, name="v_codes", align_bytes=64)
        v_scales = keep.tile([P, PASSES, P], U8, name="v_scales", align_bytes=64)
        w_planes = keep.tile([P, PASSES // 4, N], U8, name="w_planes", align_bytes=64)
        ident_f32 = keep.tile([P, P], F32, name="ident_f32")
        ident_bf16 = keep.tile([P, P], BF16, name="ident_bf16")
        first_row = keep.tile([P, P], BF16, name="first_row")
        rho_cols = keep.tile([P, P], BF16, name="rho_cols")
        rho_rows = keep.tile([P, P], BF16, name="rho_rows")
        b_rows = keep.tile([P, N], BF16, name="b_rows")
        b_all = keep.tile([P, N], BF16, name="b_all")
        z_sb = keep.tile([P, N], BF16, name="z_sb")
        mv_first = keep.tile([P, N_FIRST], F32, name="mv_first")
        w_last = keep.tile([P, BANK], F32, name="w_last")
        scrap_s = keep.tile([P, N], BF16, name="scrap_s")
        scrap_v = keep.tile([P, BANK], F32, name="scrap_v")
        step_logit = rows.tile([P, 1], BF16, name="step_logit")
        minus_half = row_value("minus_half", 2)
        tiny = row_value("tiny")

        for i in range(4):
            cols = slice(2048 * i, 2048 * (i + 1))
            nc.sync.dma_start(out=v_sb[:, cols], in_=v_init[:, cols])
        nc.vector.memset(w_planes[:].rearrange("p j n -> p (j n)").bitcast(I32), 0)
        nc.vector.memset(b_rows[:].bitcast(I32), 0)
        nc.vector.memset(first_row[:], 0.0)
        nc.vector.memset(first_row[0:1, :], 1.0)
        nc.vector.memset(rho_cols[:], 0.0)
        nc.vector.memset(minus_half[:], -0.5)
        nc.vector.memset(tiny[:], TINY)
        make_identity(nc, ident_f32[:])
        make_identity(nc, ident_bf16[:])
        nc.scalar.dma_start(out=step_logit[:], in_=step_sizes.partition_broadcast(P))
        nc.scalar.dma_start(out=b_rows[0:2, :], in_=b.partition_broadcast(2))
        for j in range(PASSES // 4):
            for quarter in range(4):
                nc.sync.dma_start(
                    out=w_planes[32 * quarter:32 * quarter + 16, j, :].bitcast(I32),
                    in_=W_scales[4 * j:4 * j + 4, 4 * quarter:4 * quarter + 4, :].bitcast(I32),
                )
        nc.sync.dma_start(out=z_sb[:], in_=z_0)

        w_tiles = []

        def load_weights(n):
            w_tile = weights.tile([P, N_FIRST], U32, name="w_tile%d" % n, tag="w_tile", align_bytes=64)
            w_tiles.append(w_tile)
            dst = w_tile[:].bitcast(I32)
            if n < PASSES:
                src = W_words[n].rearrange("p n t -> p (n t)")[:, 0:4 * N_FIRST].bitcast(I32)
                nc.sync.dma_start(out=dst, in_=src)
            else:
                g0 = 4 * (n - PASSES)
                cuts = [(0, 4)] if n < W_TILES - 1 else [(0, 2), (2, 3), (3, 4)]
                dst_by_pass = dst.rearrange("p (g c) -> p g c", g=4)
                for lo, hi in cuts:
                    src = W_words[g0 + lo:g0 + hi].rearrange("g p n t -> p g (n t)")[:, :, 4 * N_FIRST:4 * N]
                    nc.sync.dma_start(out=dst_by_pass[:, lo:hi, :], in_=src.bitcast(I32))

        for n in range(W_BUFS):
            load_weights(n)

        v_as_words = v_sb[:].bitcast(F32)
        transposed = []
        for h in range(8):
            bank = psum.tile([P, 2, 2, P], F32, name="transposed%d" % h, tag="bank%d" % h)
            transposed.append(bank)
            for i in range(2):
                g = 2 * h + i
                for u in range(2):
                    nc.tensor.transpose(bank[:, i, u, :], v_as_words[:, 256 * g + u:256 * (g + 1):2], ident_f32[:])

        def regroup(h):
            dst = v_words[:, 2 * h:2 * h + 2, :, :]
            src = transposed[h][:].rearrange("p g u r -> p g r u")
            if h % 2 == 0:
                nc.vector.tensor_copy(out=dst, in_=src)
            else:
                nc.scalar.copy(out=dst, in_=src)

        def quantise(i):
            four = slice(4 * i, 4 * i + 4)
            nc.vector.quantize_mx(
                out=v_codes[:, four, :].rearrange("p g r -> p (g r)").bitcast(FP8X4),
                scales=v_scales[:, four, :].rearrange("p g r -> p (g r)"),
                in_=v_words[:, four, :, :].rearrange("p g r u -> p (g r u)").bitcast(BF16),
            )

        regroup(0)
        regroup(1)
        for i in range(3):
            regroup(2 * i + 2)
            regroup(2 * i + 3)
            quantise(i)
        quantise(3)

        for c in range(CHUNKS):
            bank = psum.tile([P, BANK], F32, name="b_bank%d" % c, tag="bank%d" % (4 + c % 4))
            nc.tensor.matmul(bank[:], lhsT=first_row[:], rhs=b_rows[:, chunk(c)], start=True, stop=True)
            nc.scalar.copy(out=b_all[:, chunk(c)], in_=bank[:])

        vv_parts = row_value("vv_parts", 4)
        for i in range(4):
            nc.scalar.activation(out=scrap_s[:, 0:2048], in_=v_sb[:, 2048 * i:2048 * (i + 1)], func=ACT.Square,
                                 accum_out=vv_parts[:, i:i + 1])
        bb = row_value("bb")
        nc.scalar.activation(out=scrap_s[:], in_=b_all[:], func=ACT.Square, accum_out=bb[:])
        zz = row_value("zz")
        nc.scalar.activation(out=scrap_s[:], in_=z_sb[:], func=ACT.Square, accum_out=zz[:])
        zb_parts = row_value("zb_parts", CHUNKS)
        for c in range(CHUNKS):
            fused(scrap_v[:], z_sb[:, chunk(c)], ALU.mult, 1.0, ALU.mult, b_all[:, chunk(c)], total=zb_parts[:, c:c + 1])
        zb = row_value("zb")
        nc.vector.tensor_reduce(out=zb[:], in_=zb_parts[:], axis=AX.X, op=ALU.add)

        vv = row_value("vv")
        nc.vector.tensor_reduce(out=vv[:], in_=vv_parts[:], axis=AX.X, op=ALU.add)
        vv_c = row_value("vv_c")
        scal(vv_c[:], vv[:], EPS_SQ, ALU.max)
        inv_vn = row_value("inv_vn")
        inverse_root(inv_vn[:], vv_c[:])
        vn_c = row_value("vn_c")
        scal(vn_c[:], vv_c[:], inv_vn[:], ALU.mult, MAX_NORM, ALU.min)
        one_minus = row_value("one_minus")
        scal(one_minus[:], vn_c[:], -1.0, ALU.mult, 1.0, ALU.add)
        inv_one_minus = row_value("inv_one_minus")
        inverse(inv_one_minus[:], one_minus[:])
        ratio = row_value("ratio")
        fused(ratio[:], vn_c[:], ALU.add, 1.0, ALU.mult, inv_one_minus[:])
        log_ratio = row_value("log_ratio")
        nc.scalar.activation(out=log_ratio[:], in_=ratio[:], func=ACT.Ln)
        gain = row_value("gain")
        fused(gain[:], log_ratio[:], ALU.mult, 0.5, ALU.mult, inv_vn[:])

        bb_c = row_value("bb_c")
        scal(bb_c[:], bb[:], EPS_SQ, ALU.max)
        inv_bn = row_value("inv_bn")
        inverse_root(inv_bn[:], bb_c[:])
        bn = row_value("bn")
        pair(bn[:], bb_c[:], ALU.mult, inv_bn[:])
        tanh_half = row_value("tanh_half")
        nc.scalar.activation(out=tanh_half[:], in_=step_logit[:], func=ACT.Tanh, scale=0.5)
        tanh_bn = row_value("tanh_bn")
        nc.scalar.activation(out=tanh_bn[:], in_=bn[:], func=ACT.Tanh)
        beta = row_value("beta")
        pair(beta[:], tanh_bn[:], ALU.mult, inv_bn[:])
        two_beta = row_value("two_beta")
        scal(two_beta[:], beta[:], 2.0, ALU.mult)
        y2 = row_value("y2")
        fused(y2[:], beta[:], ALU.mult, beta[:], ALU.mult, bb[:])
        steps = row_value("steps", 2)
        scal(steps[:, 0:1], tanh_half[:], 0.5, ALU.mult, 0.5, ALU.add)
        scal(steps[:, 1:2], tanh_half[:], 1.0, ALU.add)
        one_minus_zz = row_value("one_minus_zz")
        scal(one_minus_zz[:], zz[:], -1.0, ALU.mult, 1.0, ALU.add)
        one_minus_zz_c = row_value("one_minus_zz_c")
        scal(one_minus_zz_c[:], one_minus_zz[:], EPS, ALU.max)
        half_lam = row_value("half_lam")
        inverse(half_lam[:], one_minus_zz_c[:])
        steps_over_eps = row_value("steps_over_eps", 2)
        scal(steps_over_eps[:], steps[:], 1.0 / EPS, ALU.mult)

        x_first = rows.tile([P, 3, 3], F32, name="x_first")
        abc_first = rows.tile([P, 3, 3], F32, name="abc_first")
        val_first = rows.tile([P, 3, 3], F32, name="val_first")
        x_second = rows.tile([P, 2, 3, 3], F32, name="x_second")
        abc_second = rows.tile([P, 2, 3, 3], F32, name="abc_second")
        val_second = rows.tile([P, 2, 3, 3], F32, name="val_second")
        nc.vector.memset(x_first[:], 0.0)
        nc.vector.memset(x_second[:], 0.0)
        nc.vector.memset(abc_first[:], 0.0)
        nc.vector.memset(abc_first[:, 0, 0:1], 1.0)
        nc.vector.memset(abc_first[:, 1, 2:3], 1.0)
        scal(abc_first[:, 1, 0:1], y2[:], 0.0, ALU.add)
        scal(abc_first[:, 0, 2:3], y2[:], 0.0, ALU.add)
        scal(abc_first[:, 2, 2:3], y2[:], 1.0, ALU.add)
        nc.vector.memset(abc_second[:], 1.0)
        scal(abc_second[:, :, 1, 2], zz[:].to_broadcast([P, 2]), 0.0, ALU.add)

        acc = []
        for c in range(CHUNKS):
            bank = psum.tile([P, BANK], F32, name="acc%d" % c, tag="bank%d" % c)
            acc.append(bank)

        def mx_pass(g, c, w_tile, col):
            nc.tensor.matmul_mx(
                out=acc[c][:],
                lhsT=v_codes[:, g, :].bitcast(FP8X4),
                lhsT_scale=v_scales[:, g, :],
                rhs=w_tile[:, col:col + BANK].bitcast(FP8X4),
                rhs_scale=w_planes[4 * (g % 4):P, g // 4, chunk(c)],
                start=(g == 0),
                stop=(g == PASSES - 1),
            )

        s_parts = row_value("s_parts", LAST)
        d_parts = row_value("d_parts", LAST)
        z_parts = row_value("z_parts", LAST)
        s_first = row_value("s_first")
        d_first = row_value("d_first")
        z_first = row_value("z_first")

        def sums_over_first_block():
            for c in range(LAST):
                nc.scalar.copy(out=mv_first[:, chunk(c)], in_=acc[c][:])
                nc.scalar.activation(out=scrap_s[:, 0:BANK], in_=acc[c][:], func=ACT.Square,
                                     accum_out=s_parts[:, c:c + 1])
                fused(scrap_v[:], mv_first[:, chunk(c)], ALU.mult, 1.0, ALU.mult, b_all[:, chunk(c)],
                      total=d_parts[:, c:c + 1])
                fused(scrap_v[:], mv_first[:, chunk(c)], ALU.mult, 1.0, ALU.mult, z_sb[:, chunk(c)],
                      total=z_parts[:, c:c + 1])
            nc.vector.tensor_reduce(out=s_first[:], in_=s_parts[:], axis=AX.X, op=ALU.add)
            nc.vector.tensor_reduce(out=d_first[:], in_=d_parts[:], axis=AX.X, op=ALU.add)
            nc.vector.tensor_reduce(out=z_first[:], in_=z_parts[:], axis=AX.X, op=ALU.add)

        for n in range(W_TILES):
            if n < PASSES:
                for c in range(LAST):
                    mx_pass(n, c, w_tiles[n], BANK * c)
            else:
                for i in range(4):
                    mx_pass(4 * (n - PASSES) + i, LAST, w_tiles[n], BANK * i)
            if n + W_BUFS < W_TILES:
                load_weights(n + W_BUFS)
            if n == PASSES - 1:
                sums_over_first_block()

        w_banks = []
        for c in range(LAST):
            bank = psum.tile([P, BANK], F32, name="w_bank%d" % c, tag="bank%d" % c)
            w_banks.append(bank)
            nc.tensor.matmul(bank[:], lhsT=ident_f32[:], rhs=mv_first[:, chunk(c)], start=True, stop=False)

        s_last = row_value("s_last")
        nc.scalar.activation(out=scrap_s[:, 0:BANK], in_=acc[LAST][:], func=ACT.Square, accum_out=s_last[:])
        s_c = row_value("s_c")
        scal(s_c[:], s_last[:], s_first[:], ALU.add, EPS_SQ, ALU.max)
        inv_m = row_value("inv_m")
        inverse_root(inv_m[:], s_c[:])
        gain_s = row_value("gain_s")
        pair(gain_s[:], s_c[:], ALU.mult, gain[:])
        nc.scalar.activation(out=x_first[:, :, 1:3], in_=inv_m[:].unsqueeze(2).to_broadcast([P, 3, 2]), func=ACT.Tanh,
                             scale=gain_s[:])
        th = x_first[:, 0, 1:2]
        d_last = row_value("d_last")
        fused(scrap_v[:], acc[LAST][:], ALU.mult, 1.0, ALU.mult, b_all[:, chunk(LAST)], total=d_last[:])
        d_beta = row_value("d_beta")
        scal(d_beta[:], d_last[:], d_first[:], ALU.add, two_beta[:], ALU.mult)
        scal(abc_first[:, :, 1], d_beta[:].to_broadcast([P, 3]), inv_m[:], ALU.mult)

        horner(val_first[:].rearrange("p f e -> p (f e)"), x_first[:].rearrange("p f e -> p (f e)"),
               abc_first[:].rearrange("p f e -> p (f e)"))
        norm1 = val_first[:, 0, 2:3]
        den1 = val_first[:, 1, 2:3]
        coef_x = val_first[:, 2, 2:3]
        nd1 = row_value("nd1")
        fused(nd1[:], norm1, ALU.mult, den1, ALU.max, tiny[:])
        inv_root1 = row_value("inv_root1")
        inverse_root(inv_root1[:], nd1[:])
        den1_c = row_value("den1_c")
        scal(den1_c[:], den1, EPS, ALU.max)
        alpha = row_value("alpha")
        pair(alpha[:], th, ALU.mult, inv_m[:])
        one_minus_x2 = row_value("one_minus_x2")
        pair(one_minus_x2[:], coef_x, ALU.subtract, norm1)
        inv_den1 = row_value("inv_den1")
        inverse(inv_den1[:], den1_c[:])
        e1 = row_value("e1")
        pair(e1[:], coef_x, ALU.mult, alpha[:])
        e2 = row_value("e2")
        pair(e2[:], one_minus_x2[:], ALU.mult, beta[:])
        nd1_over_den = row_value("nd1_over_den")
        pair(nd1_over_den[:], nd1[:], ALU.mult, inv_den1[:])
        inv_e1 = row_value("inv_e1")
        inverse(inv_e1[:], e1[:])
        e1_z_first = row_value("e1_z_first")
        pair(e1_z_first[:], e1[:], ALU.mult, z_first[:])
        e1_q = row_value("e1_q")
        pair(e1_q[:], e1[:], ALU.mult, one_minus_zz[:])
        rho = row_value("rho")
        pair(rho[:], e2[:], ALU.mult, inv_e1[:])
        pair(rho_cols[:, 0:1], e2[:], ALU.mult, inv_e1[:])
        z_num_first = row_value("z_num_first")
        fused(z_num_first[:], e2[:], ALU.mult, zb[:], ALU.add, e1_z_first[:])
        pair(rho_cols[:, 1:2], rho[:], ALU.subtract, rho_cols[:, 0:1])
        z_last = row_value("z_last")
        fused(scrap_v[:], acc[LAST][:], ALU.mult, 1.0, ALU.mult, z_sb[:, chunk(LAST)], total=z_last[:])
        rho_bank = psum.tile([P, P], BF16, name="rho_bank", tag="bank5")
        nc.tensor.transpose(rho_bank[:], rho_cols[:], ident_bf16[:])

        v0_norm = row_value("v0_norm")
        scal(v0_norm[:], inv_root1[:], nd1_over_den[:], ALU.mult, MAX_NORM, ALU.min)
        inv_v0 = row_value("inv_v0")
        scal(inv_v0[:], inv_root1[:], den1_c[:], ALU.mult, 1.0 / MAX_NORM, ALU.max)
        scale1 = row_value("scale1")
        fused(scale1[:], inv_root1[:], ALU.mult, MAX_NORM, ALU.min, inv_den1[:])
        z_num = row_value("z_num")
        fused(z_num[:], z_last[:], ALU.mult, e1[:], ALU.add, z_num_first[:])
        vt_norm = row_value("vt_norm", 2)
        scal(vt_norm[:], steps[:], v0_norm[:], ALU.mult, EPS, ALU.max)
        nc.scalar.activation(out=x_second[:, :, :, 1:3],
                             in_=vt_norm[:].unsqueeze(2).unsqueeze(3).to_broadcast([P, 2, 3, 2]),
                             func=ACT.Tanh, scale=half_lam[:])
        tht = x_second[:, :, 0, 1]

        gamma_v0 = row_value("gamma_v0", 2)
        scal(gamma_v0[:], steps_over_eps[:], v0_norm[:], ALU.mult, 1.0, ALU.min)
        gamma = row_value("gamma", 2)
        scal(gamma[:], steps_over_eps[:], inv_v0[:], ALU.min)
        two_z_v0 = row_value("two_z_v0")
        fused(two_z_v0[:], z_num[:], ALU.mult, 2.0, ALU.mult, scale1[:])
        scale1_e1_q = row_value("scale1_e1_q")
        pair(scale1_e1_q[:], scale1[:], ALU.mult, e1_q[:])
        twice = gamma_v0[:].unsqueeze(2).to_broadcast([P, 2, 2])
        pair(abc_second[:, :, 0:2, 0], twice, ALU.mult, twice)
        fused(abc_second[:, :, 2, 0], gamma_v0[:], ALU.mult, zz[:], ALU.mult, gamma_v0[:])
        scal(abc_second[:, :, :, 1], gamma[:].unsqueeze(2).to_broadcast([P, 2, 3]), two_z_v0[:], ALU.mult)
        g_over_tht = row_value("g_over_tht", 2)
        scal(g_over_tht[:], gamma[:], scale1_e1_q[:], ALU.mult, TINY, ALU.add)
        inv_g_over_tht = row_value("inv_g_over_tht", 2)
        inverse(inv_g_over_tht[:], g_over_tht[:])
        nc.vector.tensor_copy(out=rho_rows[:], in_=rho_bank[:])
        for c in range(LAST):
            nc.tensor.matmul(w_banks[c][:], lhsT=rho_rows[:], rhs=b_rows[:, chunk(c)], start=False, stop=True)

        horner(val_second[:].rearrange("p t f e -> p (t f e)"), x_second[:].rearrange("p t f e -> p (t f e)"),
               abc_second[:].rearrange("p t f e -> p (t f e)"))
        inv_tht = row_value("inv_tht", 2)
        inverse(inv_tht[:], tht)
        j_t = row_value("j_t", 2)
        nd2 = row_value("nd2", 2)
        for t in range(2):
            fused(j_t[:, t:t + 1], val_second[:, t, 0, 2:3], ALU.mult, inv_tht[:, t:t + 1], ALU.mult,
                  inv_g_over_tht[:, t:t + 1])
        for t in range(2):
            fused(nd2[:, t:t + 1], val_second[:, t, 1, 2:3], ALU.mult, val_second[:, t, 2, 2:3], ALU.max, tiny[:])
        inv_root2 = row_value("inv_root2", 2)
        inverse_root(inv_root2[:], nd2[:], cols=2)
        den2_c = row_value("den2_c", 2)
        scal(den2_c[:], val_second[:, :, 2, 2], EPS, ALU.max)
        g_t = row_value("g_t", 2)
        pair(g_t[:], tht, ALU.mult, g_over_tht[:])
        inv_den2 = row_value("inv_den2", 2)
        inverse(inv_den2[:], den2_c[:])
        scale2 = row_value("scale2", 2)
        a_t = row_value("a_t", 2)

        for c in range(CHUNKS):
            if c == LAST:
                fused(w_last[:], b_all[:, chunk(LAST)], ALU.mult, rho[:], ALU.add, acc[LAST][:])
            for t in range(2):
                sum_t = unscaled.tile([P, BANK], F32, name="sum%d_%d" % (c, t), tag="sum")
                w = w_banks[c][:] if c < LAST else w_last[:]
                fused(sum_t[:], z_sb[:, chunk(c)], ALU.mult, j_t[:, t:t + 1], ALU.add, w)
                if c == 0 and t == 0:
                    fused(scale2[:], inv_root2[:], ALU.mult, MAX_NORM, ALU.min, inv_den2[:])
                    pair(a_t[:], scale2[:], ALU.mult, g_t[:])
                out_t = scaled.tile([P, BANK], F32, name="out%d_%d" % (c, t), tag="out")
                nc.scalar.activation(out=out_t[:], in_=sum_t[:], func=ACT.Copy, scale=a_t[:, t:t + 1])
                nc.sync.dma_start(out=out[:, t, chunk(c)], in_=out_t[:])
